import numpy as np
import ml_dtypes


def mxq(x, axis, fmt="e4m3"):
    dtype, down = {"e4m3": (ml_dtypes.float8_e4m3fn, 7), "e5m2": (ml_dtypes.float8_e5m2, 14)}[fmt]
    v = np.moveaxis(np.asarray(x, np.float32).astype(ml_dtypes.bfloat16).astype(np.float64), axis, -1)
    blocks = v.reshape(v.shape[:-1] + (-1, 32))
    amax = np.abs(blocks).max(-1, keepdims=True)
    byte = np.maximum(np.where(amax > 0, np.frexp(amax)[1] - 1 + 127, 0) - down, 1)
    scale = np.exp2(byte - 127.0)
    codes = (blocks / scale).astype(np.float32).astype(dtype).astype(np.float64)
    return np.moveaxis((codes * scale).reshape(v.shape), -1, axis)


WIDE = False


def mx_kscale(k):
    if not WIDE:
        return np.ones(k)
    levels = np.array([10, -10, 5, -5, 0])
    a = np.random.permutation(np.resize(levels, k // 512 * 4)).reshape(k // 512, 4)
    idx = np.arange(k)
    return np.exp2(a[idx // 512, idx % 128 // 32])


BF16 = ml_dtypes.bfloat16


def bf(x):
    return np.asarray(x, np.float32).astype(BF16)


def f64(x):
    return np.asarray(x).astype(np.float64)


B, L, D, E, S = 2, 512, 1024, 2048, 128
F = E + E + S
LN_EPS = 1e-5
GQ = 1.75 * np.sqrt(np.sqrt(10.0 * L / S))


def silu(v):
    return v / (1.0 + np.exp(-v))


def setup_inputs():
    n = np.random.standard_normal
    s = mx_kscale(D)
    return {"x": bf(0.7 * n((B, L, D)) + 0.3 * n((B, L, 1))),
            "ln_g": bf((1.0 + 0.1 * n(D)) * s),
            "ln_b": bf(0.1 * n(D) * s),
            "W_in": bf(n((D, F)) / np.sqrt(D) / s[:, None]),
            "b_in": bf(0.2 * n(F)),
            "gamma_q": bf(GQ * (1.0 + 0.1 * n(S))),
            "beta_q": bf(GQ * (-0.2 + 0.1 * n(S))),
            "gamma_k": bf(GQ * (1.0 + 0.1 * n(S))),
            "beta_k": bf(GQ * (-0.2 + 0.1 * n(S)))}


def reference(x, ln_g, ln_b, W_in, b_in, gamma_q, beta_q, gamma_k, beta_k):
    x = f64(x)
    mu = x.mean(-1, keepdims=True)
    var = np.square(x - mu).mean(-1, keepdims=True)
    xn = (x - mu) / np.sqrt(var + LN_EPS) * f64(ln_g) + f64(ln_b)
    uvz = silu((mxq(xn, 2, "e4m3") @ mxq(f64(W_in), 0, "e4m3")) + f64(b_in))
    u, v, z = uvz[..., :E], uvz[..., E:E + E], uvz[..., E + E:]
    q = z * f64(gamma_q) + f64(beta_q)
    k = z * f64(gamma_k) + f64(beta_k)
    return u, v, q, k

@@ -1,0 +1,296 @@
+from contextlib import ExitStack
+
+import concourse.mybir as mybir
+from concourse.masks import make_identity
+
+F32 = mybir.dt.float32
+BF16 = mybir.dt.bfloat16
+U32 = mybir.dt.uint32
+U8 = mybir.dt.uint8
+I32 = mybir.dt.int32
+FP8X4 = mybir.dt.float8_e4m3fn_x4
+ALU = mybir.AluOpType
+ACT = mybir.ActivationFunctionType
+
+P = 128
+ROWS = 1024
+D = 1024
+E = 2048
+S = 128
+F = E + E + S
+MT = ROWS // P
+CH = 1024
+NCH = (E + E) // CH
+LN_EPS = 1e-5
+FLOPS = 2 * ROWS * D * F
+
+YBUFS = 5
+WGBUFS = 4
+OBUFS = 6
+WENG = [
+    [["S", "V"], ["S", "V"]],
+    [["G", "G"], ["G", "G"]],
+    [["G", "G"], ["G", "G"]],
+    [["G", "G"], ["G", "G"]],
+]
+NORM_ENG = ["G", "S", "G", "S", "G", "G", "G", "G"]
+EVAC_ENG = ["S", "S", "S", "S"]
+XG_ENG = "V"
+
+
+def tile_gaublock_pb_kernel(
+    tc, x, ln_g, ln_b, W_in, b_in, gamma_q, beta_q, gamma_k, beta_k, out_0, out_1, out_2, out_3
+):
+    nc = tc.nc
+    xv = x.flatten_outer_dims().rearrange("(p m) k -> p m k", m=MT)
+    wv = W_in.rearrange("(j p) n -> p j n", p=P)
+    uv = [
+        out_0.flatten_outer_dims().rearrange("(p m) f -> p m f", m=MT),
+        out_1.flatten_outer_dims().rearrange("(p m) f -> p m f", m=MT),
+    ]
+    qkv = [
+        out_2.flatten_outer_dims().rearrange("(p m) s -> p m s", m=MT),
+        out_3.flatten_outer_dims().rearrange("(p m) s -> p m s", m=MT),
+    ]
+
+    with ExitStack() as ctx:
+        const = ctx.enter_context(tc.tile_pool(name="const", bufs=1))
+        small = ctx.enter_context(tc.tile_pool(name="small", bufs=2))
+        ypool = ctx.enter_context(tc.tile_pool(name="ypool", bufs=YBUFS))
+        xstage = ctx.enter_context(tc.tile_pool(name="xstage", bufs=2))
+        wgrp = ctx.enter_context(tc.tile_pool(name="wgrp", bufs=WGBUFS))
+        opool = ctx.enter_context(tc.tile_pool(name="opool", bufs=OBUFS))
+        psum = ctx.enter_context(tc.psum_pool(name="psum", bufs=8))
+
+        prm = const.tile([P, P], BF16, name="prm")
+        nc.vector.memset(prm[:].bitcast(I32), 0)
+        nc.scalar.dma_start(out=prm[0:8, :], in_=ln_g.rearrange("(j p) -> j p", p=P))
+        nc.scalar.dma_start(out=prm[8:16, :], in_=ln_b.rearrange("(j p) -> j p", p=P))
+        mhalf = const.tile([P, 4], F32, name="mhalf")
+        nc.vector.memset(mhalf[:], -0.5)
+        ident_f = const.tile([P, P], F32, name="ident_f")
+        make_identity(nc, ident_f[:])
+        ident_b = const.tile([P, P], BF16, name="ident_b")
+        nc.vector.tensor_copy(out=ident_b[:], in_=ident_f[:])
+
+        xs = const.tile([P, MT, D], BF16, name="xs")
+        raws = {}
+        bias_bc = const.tile([P, F], BF16, name="bias_bc")
+        qk_bc = const.tile([P, 4, S], BF16, name="qk_bc")
+        zraw = const.tile([P, 8, S], BF16, name="zraw")
+
+        def load_x(i):
+            nc.sync.dma_start(out=xs[:, 2 * i : 2 * i + 2, :], in_=xv[:, 2 * i : 2 * i + 2, :])
+
+        def load_w(ch, c):
+            raw = const.tile([P, 4, CH], BF16, name="raw%d_%d" % (ch, c))
+            nc.sync.dma_start(out=raw[:], in_=wv[:, 4 * c : 4 * c + 4, CH * ch : CH * (ch + 1)])
+            raws[(ch, c)] = raw
+
+        load_x(0)
+        load_x(1)
+        load_w(0, 0)
+        load_w(0, 1)
+        load_x(2)
+        load_x(3)
+        nc.sync.dma_start(out=bias_bc[:], in_=b_in.partition_broadcast(P))
+        for ch in range(1, NCH):
+            load_w(ch, 0)
+            load_w(ch, 1)
+        nc.sync.dma_start(out=zraw[:], in_=wv[:, :, 2 * E : F])
+        for i, vec in enumerate([gamma_q, beta_q, gamma_k, beta_k]):
+            nc.sync.dma_start(out=qk_bc[:, i, :], in_=vec.partition_broadcast(P))
+
+        gb_ps = psum.tile([P, P], F32, name="gb_ps", tag="ps")
+        nc.tensor.matmul(out=gb_ps[:], lhsT=prm[:], rhs=ident_b[:], start=True, stop=True)
+        gb = const.tile([P, 16], F32, name="gb")
+        nc.vector.tensor_copy(out=gb[:], in_=gb_ps[:, 0:16])
+
+        xcodes = const.tile([P, 2, 2, 512], U32, name="xcodes", align_bytes=64)
+        xscales = const.tile([P, 2, 2, 512], U8, name="xscales", align_bytes=64)
+        wcodes = const.tile([P, 2, 2 * E], U32, name="wcodes", align_bytes=64)
+        wscales = const.tile([P, 2, 2 * E], U8, name="wscales", align_bytes=64)
+        zcodes = const.tile([P, 2, S], U32, name="zcodes", align_bytes=64)
+        zscales = const.tile([P, 2, S], U8, name="zscales", align_bytes=64)
+
+        def regroup(eng, dst, src):
+            if eng == "G":
+                nc.gpsimd.tensor_scalar(
+                    out=dst, in0=src.rearrange("p t n -> p n t"), scalar1=1.0, scalar2=0.0, op0=ALU.mult, op1=ALU.add
+                )
+            else:
+                d4 = dst.rearrange("p (c i) t -> p c t i", i=4)
+                s4 = src.rearrange("p t (c i) -> p c t i", i=4)
+                if eng == "V":
+                    nc.vector.tensor_copy(out=d4, in_=s4)
+                else:
+                    nc.scalar.copy(out=d4, in_=s4)
+
+        ln_state = {}
+
+        def ln_stats(g):
+            stats = small.tile([P, 4, 2, 6], F32, name="stats")
+            mv = small.tile([P, 4, 2], F32, name="mv")
+            for i in range(4):
+                for h in range(2):
+                    nc.vector.bn_stats(out=stats[:, i, h, :], in_=xs[:, 4 * g + i, 512 * h : 512 * h + 512])
+                nc.vector.bn_aggr(out=mv[:, i, :], in_=stats[:, i, :, :].rearrange("p a b -> p (a b)"))
+            ve = small.tile([P, 4], F32, name="ve")
+            nc.vector.tensor_scalar_add(out=ve[:], in0=mv[:, :, 1], scalar1=LN_EPS)
+            nmu = small.tile([P, 4], F32, name="nmu")
+            nc.vector.tensor_scalar_mul(out=nmu[:], in0=mv[:, :, 0], scalar1=-1.0)
+            rstd = small.tile([P, 4], F32, name="rstd")
+            nc.gpsimd.tensor_tensor(out=rstd[:], in0=ve[:], in1=mhalf[:], op=ALU.pow)
+            nmr = small.tile([P, 4], F32, name="nmr")
+            nc.gpsimd.tensor_tensor(out=nmr[:], in0=nmu[:], in1=rstd[:], op=ALU.mult)
+            ys = []
+            for i in range(4):
+                m = 4 * g + i
+                y = ypool.tile([P, D], F32, name="y")
+                if NORM_ENG[m] == "G":
+                    nc.gpsimd.tensor_scalar(
+                        out=y[:],
+                        in0=xs[:, m, :],
+                        scalar1=nmu[:, i : i + 1],
+                        scalar2=rstd[:, i : i + 1],
+                        op0=ALU.add,
+                        op1=ALU.mult,
+                    )
+                else:
+                    nc.scalar.activation(
+                        out=y[:], in_=xs[:, m, :], func=ACT.Identity, scale=rstd[:, i : i + 1], bias=nmr[:, i : i + 1]
+                    )
+                ys.append(y)
+            ln_state[g] = ys
+
+        def ln_finish(g, c):
+            ys = ln_state[g]
+            planes = xstage.tile([P, 4, 512], BF16, name="planes")
+            xts = []
+            for t in range(4):
+                xts.append(psum.tile([P, 512], F32, name="xt", tag="ps"))
+            for i in range(4):
+                for t in range(4):
+                    j = 4 * c + t
+                    nc.tensor.transpose(
+                        out=xts[t][:, P * i : P * i + P], in_=ys[i][:, P * j : P * j + P], identity=ident_f[:]
+                    )
+            for t in range(4):
+                j = 4 * c + t
+                if EVAC_ENG[t] == "S":
+                    nc.scalar.activation(
+                        out=planes[:, t, :], in_=xts[t][:], func=ACT.Identity, scale=gb[:, j : j + 1], bias=gb[:, 8 + j : 9 + j]
+                    )
+                else:
+                    nc.vector.tensor_scalar(
+                        out=planes[:, t, :],
+                        in0=xts[t][:],
+                        scalar1=gb[:, j : j + 1],
+                        scalar2=gb[:, 8 + j : 9 + j],
+                        op0=ALU.mult,
+                        op1=ALU.add,
+                    )
+            xg = xstage.tile([P, 512, 4], BF16, name="xg", align_bytes=64)
+            regroup(XG_ENG, xg[:], planes[:])
+            nc.vector.quantize_mx(
+                out=xcodes[:, g, c, :].bitcast(FP8X4), scales=xscales[:, g, c, :], in_=xg[:].rearrange("p r t -> p (r t)")
+            )
+
+        def quantise_z():
+            zg = const.tile([P, 2, S, 4], BF16, name="zg", align_bytes=64)
+            for c in range(2):
+                regroup("S", zg[:, c, :, :], zraw[:, 4 * c : 4 * c + 4, :])
+            nc.vector.quantize_mx(
+                out=zcodes[:].rearrange("p c r -> p (c r)").bitcast(FP8X4),
+                scales=zscales[:].rearrange("p c r -> p (c r)"),
+                in_=zg[:].rearrange("p c r t -> p (c r t)"),
+            )
+
+        def quantise_chunk(ch):
+            for c in range(2):
+                raw = raws[(ch, c)]
+                for h in range(2):
+                    wg = wgrp.tile([P, 512, 4], BF16, name="wg", align_bytes=64)
+                    regroup(WENG[ch][c][h], wg[:], raw[:, :, 512 * h : 512 * h + 512])
+                    n0 = CH * ch + 512 * h
+                    nc.vector.quantize_mx(
+                        out=wcodes[:, c, n0 : n0 + 512].bitcast(FP8X4),
+                        scales=wscales[:, c, n0 : n0 + 512],
+                        in_=wg[:].rearrange("p n t -> p (n t)"),
+                    )
+
+        def produce(ch, m):
+            g, i = m // 4, m % 4
+            ot = opool.tile([P, CH], F32, name="ot")
+            for h in range(2):
+                n0 = CH * ch + 512 * h
+                acc = psum.tile([P, 512], F32, name="acc", tag="ps")
+                for c in range(2):
+                    nc.tensor.matmul_mx(
+                        out=acc[:],
+                        lhsT=xcodes[:, g, c, P * i : P * i + P].bitcast(FP8X4),
+                        lhsT_scale=xscales[:, g, c, P * i : P * i + P],
+                        rhs=wcodes[:, c, n0 : n0 + 512].bitcast(FP8X4),
+                        rhs_scale=wscales[:, c, n0 : n0 + 512],
+                        start=(c == 0),
+                        stop=(c == 1),
+                    )
+                nc.vector.tensor_tensor(
+                    out=ot[:, 512 * h : 512 * h + 512], in0=acc[:], in1=bias_bc[:, n0 : n0 + 512], op=ALU.add
+                )
+            nc.scalar.activation(out=ot[:], in_=ot[:], func=ACT.Silu)
+            col = (CH * ch) % E
+            nc.sync.dma_start(out=uv[(CH * ch) // E][:, m, col : col + CH], in_=ot[:])
+
+        def produce_z():
+            zt = opool.tile([P, MT, S], F32, name="zt", tag="ot")
+            for g in range(2):
+                acc = psum.tile([P, 4, S], F32, name="accz", tag="ps")
+                for i in range(4):
+                    for c in range(2):
+                        nc.tensor.matmul_mx(
+                            out=acc[:, i, :],
+                            lhsT=xcodes[:, g, c, P * i : P * i + P].bitcast(FP8X4),
+                            lhsT_scale=xscales[:, g, c, P * i : P * i + P],
+                            rhs=zcodes[:, c, :].bitcast(FP8X4),
+                            rhs_scale=zscales[:, c, :],
+                            start=(c == 0),
+                            stop=(c == 1),
+                        )
+                nc.vector.tensor_tensor(
+                    out=zt[:, 4 * g : 4 * g + 4, :],
+                    in0=acc[:],
+                    in1=bias_bc[:, 2 * E : F].unsqueeze(1).to_broadcast([P, 4, S]),
+                    op=ALU.add,
+                )
+            nc.scalar.activation(out=zt[:], in_=zt[:], func=ACT.Silu)
+            for i in range(2):
+                gam = qk_bc[:, 2 * i, :].unsqueeze(1).to_broadcast([P, MT, S])
+                bet = qk_bc[:, 2 * i + 1, :].unsqueeze(1).to_broadcast([P, MT, S])
+                qt = opool.tile([P, MT, S], F32, name="qt", tag="ot")
+                nc.gpsimd.tensor_tensor(out=qt[:], in0=zt[:], in1=gam, op=ALU.mult)
+                nc.gpsimd.tensor_tensor(out=qt[:], in0=qt[:], in1=bet, op=ALU.add)
+                nc.sync.dma_start(out=qkv[i], in_=qt[:])
+
+        ln_stats(0)
+        quantise_chunk(0)
+        ln_finish(0, 0)
+        ln_finish(0, 1)
+        ln_stats(1)
+        for m in range(4):
+            produce(0, m)
+        ln_finish(1, 0)
+        ln_finish(1, 1)
+        quantise_chunk(1)
+        for m in range(4, MT):
+            produce(0, m)
+        quantise_chunk(2)
+        for m in range(MT):
+            produce(1, m)
+        quantise_chunk(3)
+        quantise_z()
+        for m in range(MT):
+            produce(2, m)
+        produce_z()
+        for m in range(MT):
+            produce(3, m)

@@ -25,17 +25,12 @@ LN_EPS = 1e-5
 FLOPS = 2 * ROWS * D * F
 
 YBUFS = 5
-WGBUFS = 4
+WGBUFS = 2
 OBUFS = 6
-WENG = [
-    [["S", "V"], ["S", "V"]],
-    [["G", "G"], ["G", "G"]],
-    [["G", "G"], ["G", "G"]],
-    [["G", "G"], ["G", "G"]],
-]
-NORM_ENG = ["G", "S", "G", "S", "G", "G", "G", "G"]
-EVAC_ENG = ["S", "S", "S", "S"]
-XG_ENG = "V"
+SMALL_ENG = "G"
+WENG = [["VS", "SS"], ["VV", "VV"], ["SS", "VV"], ["SG", "GG"]]
+NORM_ENG = ["S", "S", "S", "G", "S", "S", "G", "G"]
+XG_ENG = ["G", "S", "V", "G"]
 
 
 def tile_gaublock_pb_kernel(
@@ -106,8 +101,8 @@ def tile_gaublock_pb_kernel(
         gb = const.tile([P, 16], F32, name="gb")
         nc.vector.tensor_copy(out=gb[:], in_=gb_ps[:, 0:16])
 
-        xcodes = const.tile([P, 2, 2, 512], U32, name="xcodes", align_bytes=64)
-        xscales = const.tile([P, 2, 2, 512], U8, name="xscales", align_bytes=64)
+        xcodes = const.tile([P, 4, 2, 256], U32, name="xcodes", align_bytes=64)
+        xscales = const.tile([P, 4, 2, 256], U8, name="xscales", align_bytes=64)
         wcodes = const.tile([P, 2, 2 * E], U32, name="wcodes", align_bytes=64)
         wscales = const.tile([P, 2, 2 * E], U8, name="wscales", align_bytes=64)
         zcodes = const.tile([P, 2, S], U32, name="zcodes", align_bytes=64)
@@ -126,26 +121,30 @@ def tile_gaublock_pb_kernel(
                 else:
                     nc.scalar.copy(out=d4, in_=s4)
 
-        ln_state = {}
+        def small_op(out, in0, s1, s2, op0, op1):
+            if SMALL_ENG == "G":
+                nc.gpsimd.tensor_scalar(out=out, in0=in0, scalar1=s1, scalar2=s2, op0=op0, op1=op1)
+            else:
+                nc.vector.tensor_scalar(out=out, in0=in0, scalar1=s1, scalar2=s2, op0=op0, op1=op1)
 
-        def ln_stats(g):
-            stats = small.tile([P, 4, 2, 6], F32, name="stats")
-            mv = small.tile([P, 4, 2], F32, name="mv")
-            for i in range(4):
+        def layer_norm(g):
+            stats = small.tile([P, 2, 2, 6], F32, name="stats")
+            mv = small.tile([P, 2, 2], F32, name="mv")
+            for i in range(2):
                 for h in range(2):
-                    nc.vector.bn_stats(out=stats[:, i, h, :], in_=xs[:, 4 * g + i, 512 * h : 512 * h + 512])
+                    nc.vector.bn_stats(out=stats[:, i, h, :], in_=xs[:, 2 * g + i, 512 * h : 512 * h + 512])
                 nc.vector.bn_aggr(out=mv[:, i, :], in_=stats[:, i, :, :].rearrange("p a b -> p (a b)"))
-            ve = small.tile([P, 4], F32, name="ve")
-            nc.vector.tensor_scalar_add(out=ve[:], in0=mv[:, :, 1], scalar1=LN_EPS)
-            nmu = small.tile([P, 4], F32, name="nmu")
-            nc.vector.tensor_scalar_mul(out=nmu[:], in0=mv[:, :, 0], scalar1=-1.0)
-            rstd = small.tile([P, 4], F32, name="rstd")
-            nc.gpsimd.tensor_tensor(out=rstd[:], in0=ve[:], in1=mhalf[:], op=ALU.pow)
-            nmr = small.tile([P, 4], F32, name="nmr")
+            ve = small.tile([P, 2], F32, name="ve")
+            small_op(ve[:], mv[:, :, 1], LN_EPS, 1.0, ALU.add, ALU.mult)
+            nmu = small.tile([P, 2], F32, name="nmu")
+            small_op(nmu[:], mv[:, :, 0], -1.0, 0.0, ALU.mult, ALU.add)
+            rstd = small.tile([P, 2], F32, name="rstd")
+            nc.gpsimd.tensor_tensor(out=rstd[:], in0=ve[:], in1=mhalf[:, 0:2], op=ALU.pow)
+            nmr = small.tile([P, 2], F32, name="nmr")
             nc.gpsimd.tensor_tensor(out=nmr[:], in0=nmu[:], in1=rstd[:], op=ALU.mult)
             ys = []
-            for i in range(4):
-                m = 4 * g + i
+            for i in range(2):
+                m = 2 * g + i
                 y = ypool.tile([P, D], F32, name="y")
                 if NORM_ENG[m] == "G":
                     nc.gpsimd.tensor_scalar(
@@ -161,39 +160,31 @@ def tile_gaublock_pb_kernel(
                         out=y[:], in_=xs[:, m, :], func=ACT.Identity, scale=rstd[:, i : i + 1], bias=nmr[:, i : i + 1]
                     )
                 ys.append(y)
-            ln_state[g] = ys
-
-        def ln_finish(g, c):
-            ys = ln_state[g]
-            planes = xstage.tile([P, 4, 512], BF16, name="planes")
-            xts = []
-            for t in range(4):
-                xts.append(psum.tile([P, 512], F32, name="xt", tag="ps"))
-            for i in range(4):
-                for t in range(4):
-                    j = 4 * c + t
-                    nc.tensor.transpose(
-                        out=xts[t][:, P * i : P * i + P], in_=ys[i][:, P * j : P * j + P], identity=ident_f[:]
-                    )
-            for t in range(4):
-                j = 4 * c + t
-                if EVAC_ENG[t] == "S":
+            planes = xstage.tile([P, 8, 256], BF16, name="planes")
+            for a in range(4):
+                xt = psum.tile([P, 2, 256], F32, name="xt", tag="ps")
+                for jj in range(2):
+                    j = 2 * a + jj
+                    for i in range(2):
+                        nc.tensor.transpose(
+                            out=xt[:, jj, P * i : P * i + P], in_=ys[i][:, P * j : P * j + P], identity=ident_f[:]
+                        )
+                for jj in range(2):
+                    j = 2 * a + jj
                     nc.scalar.activation(
-                        out=planes[:, t, :], in_=xts[t][:], func=ACT.Identity, scale=gb[:, j : j + 1], bias=gb[:, 8 + j : 9 + j]
+                        out=planes[:, j, :],
+                        in_=xt[:, jj, :],
+                        func=ACT.Identity,
+                        scale=gb[:, j : j + 1],
+                        bias=gb[:, 8 + j : 9 + j],
                     )
-                else:
-                    nc.vector.tensor_scalar(
-                        out=planes[:, t, :],
-                        in0=xts[t][:],
-                        scalar1=gb[:, j : j + 1],
-                        scalar2=gb[:, 8 + j : 9 + j],
-                        op0=ALU.mult,
-                        op1=ALU.add,
-                    )
-            xg = xstage.tile([P, 512, 4], BF16, name="xg", align_bytes=64)
-            regroup(XG_ENG, xg[:], planes[:])
+            xg = xstage.tile([P, 2, 256, 4], BF16, name="xg", align_bytes=64)
+            for c in range(2):
+                regroup(XG_ENG[g], xg[:, c, :, :], planes[:, 4 * c : 4 * c + 4, :])
             nc.vector.quantize_mx(
-                out=xcodes[:, g, c, :].bitcast(FP8X4), scales=xscales[:, g, c, :], in_=xg[:].rearrange("p r t -> p (r t)")
+                out=xcodes[:, g, :, :].rearrange("p c r -> p (c r)").bitcast(FP8X4),
+                scales=xscales[:, g, :, :].rearrange("p c r -> p (c r)"),
+                in_=xg[:].rearrange("p c r t -> p (c r t)"),
             )
 
         def quantise_z():
@@ -207,20 +198,24 @@ def tile_gaublock_pb_kernel(
             )
 
         def quantise_chunk(ch):
+            wgs = []
             for c in range(2):
                 raw = raws[(ch, c)]
-                for h in range(2):
-                    wg = wgrp.tile([P, 512, 4], BF16, name="wg", align_bytes=64)
-                    regroup(WENG[ch][c][h], wg[:], raw[:, :, 512 * h : 512 * h + 512])
-                    n0 = CH * ch + 512 * h
-                    nc.vector.quantize_mx(
-                        out=wcodes[:, c, n0 : n0 + 512].bitcast(FP8X4),
-                        scales=wscales[:, c, n0 : n0 + 512],
-                        in_=wg[:].rearrange("p n t -> p (n t)"),
-                    )
+                wg = wgrp.tile([P, CH, 4], BF16, name="wg", align_bytes=64)
+                engs = WENG[ch][c]
+                w = CH // len(engs)
+                for h, eng in enumerate(engs):
+                    regroup(eng, wg[:, w * h : w * (h + 1), :], raw[:, :, w * h : w * (h + 1)])
+                wgs.append(wg)
+            for c in range(2):
+                nc.vector.quantize_mx(
+                    out=wcodes[:, c, CH * ch : CH * (ch + 1)].bitcast(FP8X4),
+                    scales=wscales[:, c, CH * ch : CH * (ch + 1)],
+                    in_=wgs[c][:].rearrange("p n t -> p (n t)"),
+                )
 
         def produce(ch, m):
-            g, i = m // 4, m % 4
+            g, i = m // 2, m % 2
             ot = opool.tile([P, CH], F32, name="ot")
             for h in range(2):
                 n0 = CH * ch + 512 * h
@@ -247,11 +242,12 @@ def tile_gaublock_pb_kernel(
             for g in range(2):
                 acc = psum.tile([P, 4, S], F32, name="accz", tag="ps")
                 for i in range(4):
+                    pr, mm = (4 * g + i) // 2, i % 2
                     for c in range(2):
                         nc.tensor.matmul_mx(
                             out=acc[:, i, :],
-                            lhsT=xcodes[:, g, c, P * i : P * i + P].bitcast(FP8X4),
-                            lhsT_scale=xscales[:, g, c, P * i : P * i + P],
+                            lhsT=xcodes[:, pr, c, P * mm : P * mm + P].bitcast(FP8X4),
+                            lhsT_scale=xscales[:, pr, c, P * mm : P * mm + P],
                             rhs=zcodes[:, c, :].bitcast(FP8X4),
                             rhs_scale=zscales[:, c, :],
                             start=(c == 0),
@@ -272,15 +268,15 @@ def tile_gaublock_pb_kernel(
                 nc.gpsimd.tensor_tensor(out=qt[:], in0=qt[:], in1=bet, op=ALU.add)
                 nc.sync.dma_start(out=qkv[i], in_=qt[:])
 
-        ln_stats(0)
+        layer_norm(0)
         quantise_chunk(0)
-        ln_finish(0, 0)
-        ln_finish(0, 1)
-        ln_stats(1)
-        for m in range(4):
-            produce(0, m)
-        ln_finish(1, 0)
-        ln_finish(1, 1)
+        layer_norm(1)
+        produce(0, 0)
+        produce(0, 1)
+        layer_norm(2)
+        produce(0, 2)
+        produce(0, 3)
+        layer_norm(3)
         quantise_chunk(1)
         for m in range(4, MT):
             produce(0, m)

@@ -24,13 +24,12 @@ NCH = (E + E) // CH
 LN_EPS = 1e-5
 FLOPS = 2 * ROWS * D * F
 
-YBUFS = 5
-WGBUFS = 2
-OBUFS = 6
-SMALL_ENG = "G"
-WENG = [["VS", "SS"], ["VV", "VV"], ["SS", "VV"], ["SG", "GG"]]
-NORM_ENG = ["S", "S", "S", "G", "S", "S", "G", "G"]
-XG_ENG = ["G", "S", "V", "G"]
+BTBUFS = 8
+OBUFS = 8
+EV_S_EVERY = 6
+WENG = [["S", "S"], ["V", "V"], ["V", "V"], ["V", "V"]]
+NORM_ENG = ["G", "S", "G", "S", "G", "S", "G", "S"]
+XG_ENG = ["VV", "VV"]
 
 
 def tile_gaublock_pb_kernel(
@@ -51,11 +50,12 @@ def tile_gaublock_pb_kernel(
     with ExitStack() as ctx:
         const = ctx.enter_context(tc.tile_pool(name="const", bufs=1))
         small = ctx.enter_context(tc.tile_pool(name="small", bufs=2))
-        ypool = ctx.enter_context(tc.tile_pool(name="ypool", bufs=YBUFS))
+        ypool = ctx.enter_context(tc.tile_pool(name="ypool", bufs=4))
         xstage = ctx.enter_context(tc.tile_pool(name="xstage", bufs=2))
-        wgrp = ctx.enter_context(tc.tile_pool(name="wgrp", bufs=WGBUFS))
+        wgrp = ctx.enter_context(tc.tile_pool(name="wgrp", bufs=2))
+        btp = ctx.enter_context(tc.tile_pool(name="btp", bufs=BTBUFS))
         opool = ctx.enter_context(tc.tile_pool(name="opool", bufs=OBUFS))
-        psum = ctx.enter_context(tc.psum_pool(name="psum", bufs=8))
+        psum = ctx.enter_context(tc.psum_pool(name="psum", bufs=4))
 
         prm = const.tile([P, P], BF16, name="prm")
         nc.vector.memset(prm[:].bitcast(I32), 0)
@@ -70,8 +70,6 @@ def tile_gaublock_pb_kernel(
 
         xs = const.tile([P, MT, D], BF16, name="xs")
         raws = {}
-        bias_bc = const.tile([P, F], BF16, name="bias_bc")
-        qk_bc = const.tile([P, 4, S], BF16, name="qk_bc")
         zraw = const.tile([P, 8, S], BF16, name="zraw")
 
         def load_x(i):
@@ -88,21 +86,21 @@ def tile_gaublock_pb_kernel(
         load_w(0, 1)
         load_x(2)
         load_x(3)
-        nc.sync.dma_start(out=bias_bc[:], in_=b_in.partition_broadcast(P))
+        nc.scalar.dma_start(out=prm[16:49, :], in_=b_in.rearrange("(j p) -> j p", p=P))
+        for i, vec in enumerate([gamma_q, beta_q, gamma_k, beta_k]):
+            nc.scalar.dma_start(out=prm[49 + i : 50 + i, :], in_=vec.unsqueeze(0))
         for ch in range(1, NCH):
             load_w(ch, 0)
             load_w(ch, 1)
         nc.sync.dma_start(out=zraw[:], in_=wv[:, :, 2 * E : F])
-        for i, vec in enumerate([gamma_q, beta_q, gamma_k, beta_k]):
-            nc.sync.dma_start(out=qk_bc[:, i, :], in_=vec.partition_broadcast(P))
 
-        gb_ps = psum.tile([P, P], F32, name="gb_ps", tag="ps")
-        nc.tensor.matmul(out=gb_ps[:], lhsT=prm[:], rhs=ident_b[:], start=True, stop=True)
-        gb = const.tile([P, 16], F32, name="gb")
-        nc.vector.tensor_copy(out=gb[:], in_=gb_ps[:, 0:16])
+        pc_ps = psum.tile([P, P], F32, name="pc_ps", tag="tb")
+        nc.tensor.matmul(out=pc_ps[:], lhsT=prm[:], rhs=ident_b[:], start=True, stop=True)
+        pc = const.tile([P, 64], F32, name="pc")
+        nc.vector.tensor_copy(out=pc[:], in_=pc_ps[:, 0:64])
 
-        xcodes = const.tile([P, 4, 2, 256], U32, name="xcodes", align_bytes=64)
-        xscales = const.tile([P, 4, 2, 256], U8, name="xscales", align_bytes=64)
+        xcodes = const.tile([P, 2, 2, 512], U32, name="xcodes", align_bytes=64)
+        xscales = const.tile([P, 2, 2, 512], U8, name="xscales", align_bytes=64)
         wcodes = const.tile([P, 2, 2 * E], U32, name="wcodes", align_bytes=64)
         wscales = const.tile([P, 2, 2 * E], U8, name="wscales", align_bytes=64)
         zcodes = const.tile([P, 2, S], U32, name="zcodes", align_bytes=64)
@@ -121,30 +119,32 @@ def tile_gaublock_pb_kernel(
                 else:
                     nc.scalar.copy(out=d4, in_=s4)
 
-        def small_op(out, in0, s1, s2, op0, op1):
-            if SMALL_ENG == "G":
-                nc.gpsimd.tensor_scalar(out=out, in0=in0, scalar1=s1, scalar2=s2, op0=op0, op1=op1)
+        def leave_psum(eng, dst, src):
+            if eng == "V":
+                nc.vector.tensor_copy(out=dst, in_=src)
             else:
-                nc.vector.tensor_scalar(out=out, in0=in0, scalar1=s1, scalar2=s2, op0=op0, op1=op1)
+                nc.scalar.copy(out=dst, in_=src)
 
-        def layer_norm(g):
-            stats = small.tile([P, 2, 2, 6], F32, name="stats")
-            mv = small.tile([P, 2, 2], F32, name="mv")
-            for i in range(2):
+        ln_state = {}
+
+        def ln_stats(g):
+            stats = small.tile([P, 4, 2, 6], F32, name="stats")
+            mv = small.tile([P, 4, 2], F32, name="mv")
+            for i in range(4):
                 for h in range(2):
-                    nc.vector.bn_stats(out=stats[:, i, h, :], in_=xs[:, 2 * g + i, 512 * h : 512 * h + 512])
+                    nc.vector.bn_stats(out=stats[:, i, h, :], in_=xs[:, 4 * g + i, 512 * h : 512 * h + 512])
                 nc.vector.bn_aggr(out=mv[:, i, :], in_=stats[:, i, :, :].rearrange("p a b -> p (a b)"))
-            ve = small.tile([P, 2], F32, name="ve")
-            small_op(ve[:], mv[:, :, 1], LN_EPS, 1.0, ALU.add, ALU.mult)
-            nmu = small.tile([P, 2], F32, name="nmu")
-            small_op(nmu[:], mv[:, :, 0], -1.0, 0.0, ALU.mult, ALU.add)
-            rstd = small.tile([P, 2], F32, name="rstd")
-            nc.gpsimd.tensor_tensor(out=rstd[:], in0=ve[:], in1=mhalf[:, 0:2], op=ALU.pow)
-            nmr = small.tile([P, 2], F32, name="nmr")
+            ve = small.tile([P, 4], F32, name="ve")
+            nc.gpsimd.tensor_scalar(out=ve[:], in0=mv[:, :, 1], scalar1=LN_EPS, scalar2=1.0, op0=ALU.add, op1=ALU.mult)
+            nmu = small.tile([P, 4], F32, name="nmu")
+            nc.gpsimd.tensor_scalar(out=nmu[:], in0=mv[:, :, 0], scalar1=-1.0, scalar2=0.0, op0=ALU.mult, op1=ALU.add)
+            rstd = small.tile([P, 4], F32, name="rstd")
+            nc.gpsimd.tensor_tensor(out=rstd[:], in0=ve[:], in1=mhalf[:], op=ALU.pow)
+            nmr = small.tile([P, 4], F32, name="nmr")
             nc.gpsimd.tensor_tensor(out=nmr[:], in0=nmu[:], in1=rstd[:], op=ALU.mult)
             ys = []
-            for i in range(2):
-                m = 2 * g + i
+            for i in range(4):
+                m = 4 * g + i
                 y = ypool.tile([P, D], F32, name="y")
                 if NORM_ENG[m] == "G":
                     nc.gpsimd.tensor_scalar(
@@ -160,27 +160,28 @@ def tile_gaublock_pb_kernel(
                         out=y[:], in_=xs[:, m, :], func=ACT.Identity, scale=rstd[:, i : i + 1], bias=nmr[:, i : i + 1]
                     )
                 ys.append(y)
-            planes = xstage.tile([P, 8, 256], BF16, name="planes")
-            for a in range(4):
-                xt = psum.tile([P, 2, 256], F32, name="xt", tag="ps")
-                for jj in range(2):
-                    j = 2 * a + jj
-                    for i in range(2):
-                        nc.tensor.transpose(
-                            out=xt[:, jj, P * i : P * i + P], in_=ys[i][:, P * j : P * j + P], identity=ident_f[:]
-                        )
-                for jj in range(2):
-                    j = 2 * a + jj
-                    nc.scalar.activation(
-                        out=planes[:, j, :],
-                        in_=xt[:, jj, :],
-                        func=ACT.Identity,
-                        scale=gb[:, j : j + 1],
-                        bias=gb[:, 8 + j : 9 + j],
-                    )
-            xg = xstage.tile([P, 2, 256, 4], BF16, name="xg", align_bytes=64)
+            ln_state[g] = ys
+
+        def ln_finish(g):
+            ys = ln_state[g]
+            xg = xstage.tile([P, 2, 512, 4], BF16, name="xg", align_bytes=64, bufs=1)
             for c in range(2):
-                regroup(XG_ENG[g], xg[:, c, :, :], planes[:, 4 * c : 4 * c + 4, :])
+                planes = xstage.tile([P, 4, 512], BF16, name="planes")
+                xts = []
+                for t in range(4):
+                    xts.append(psum.tile([P, 512], F32, name="xt", tag="tb"))
+                for i in range(4):
+                    for t in range(4):
+                        j = 4 * c + t
+                        nc.tensor.transpose(
+                            out=xts[t][:, P * i : P * i + P], in_=ys[i][:, P * j : P * j + P], identity=ident_f[:]
+                        )
+                for t in range(4):
+                    j = 4 * c + t
+                    nc.scalar.activation(
+                        out=planes[:, t, :], in_=xts[t][:], func=ACT.Identity, scale=pc[:, j : j + 1], bias=pc[:, 8 + j : 9 + j]
+                    )
+                regroup(XG_ENG[g][c], xg[:, c, :, :], planes[:])
             nc.vector.quantize_mx(
                 out=xcodes[:, g, :, :].rearrange("p c r -> p (c r)").bitcast(FP8X4),
                 scales=xscales[:, g, :, :].rearrange("p c r -> p (c r)"),
@@ -190,7 +191,7 @@ def tile_gaublock_pb_kernel(
         def quantise_z():
             zg = const.tile([P, 2, S, 4], BF16, name="zg", align_bytes=64)
             for c in range(2):
-                regroup("S", zg[:, c, :, :], zraw[:, 4 * c : 4 * c + 4, :])
+                regroup("V", zg[:, c, :, :], zraw[:, 4 * c : 4 * c + 4, :])
             nc.vector.quantize_mx(
                 out=zcodes[:].rearrange("p c r -> p (c r)").bitcast(FP8X4),
                 scales=zscales[:].rearrange("p c r -> p (c r)"),
@@ -198,7 +199,6 @@ def tile_gaublock_pb_kernel(
             )
 
         def quantise_chunk(ch):
-            wgs = []
             for c in range(2):
                 raw = raws[(ch, c)]
                 wg = wgrp.tile([P, CH, 4], BF16, name="wg", align_bytes=64)
@@ -206,87 +206,102 @@ def tile_gaublock_pb_kernel(
                 w = CH // len(engs)
                 for h, eng in enumerate(engs):
                     regroup(eng, wg[:, w * h : w * (h + 1), :], raw[:, :, w * h : w * (h + 1)])
-                wgs.append(wg)
-            for c in range(2):
                 nc.vector.quantize_mx(
                     out=wcodes[:, c, CH * ch : CH * (ch + 1)].bitcast(FP8X4),
                     scales=wscales[:, c, CH * ch : CH * (ch + 1)],
-                    in_=wgs[c][:].rearrange("p n t -> p (n t)"),
+                    in_=wg[:].rearrange("p n t -> p (n t)"),
                 )
 
-        def produce(ch, m):
-            g, i = m // 2, m % 2
-            ot = opool.tile([P, CH], F32, name="ot")
-            for h in range(2):
-                n0 = CH * ch + 512 * h
-                acc = psum.tile([P, 512], F32, name="acc", tag="ps")
+        bts = {}
+        count = [0]
+
+        def multiply(n0, g):
+            tiles = []
+            for fb in range(4):
+                acc = psum.tile([P, 512], F32, name="acc", tag="acc")
                 for c in range(2):
                     nc.tensor.matmul_mx(
                         out=acc[:],
-                        lhsT=xcodes[:, g, c, P * i : P * i + P].bitcast(FP8X4),
-                        lhsT_scale=xscales[:, g, c, P * i : P * i + P],
-                        rhs=wcodes[:, c, n0 : n0 + 512].bitcast(FP8X4),
-                        rhs_scale=wscales[:, c, n0 : n0 + 512],
+                        lhsT=wcodes[:, c, n0 + P * fb : n0 + P * fb + P].bitcast(FP8X4),
+                        lhsT_scale=wscales[:, c, n0 + P * fb : n0 + P * fb + P],
+                        rhs=xcodes[:, g, c, :].bitcast(FP8X4),
+                        rhs_scale=xscales[:, g, c, :],
                         start=(c == 0),
                         stop=(c == 1),
                     )
-                nc.vector.tensor_tensor(
-                    out=ot[:, 512 * h : 512 * h + 512], in0=acc[:], in1=bias_bc[:, n0 : n0 + 512], op=ALU.add
-                )
-            nc.scalar.activation(out=ot[:], in_=ot[:], func=ACT.Silu)
-            col = (CH * ch) % E
-            nc.sync.dma_start(out=uv[(CH * ch) // E][:, m, col : col + CH], in_=ot[:])
+                bt = btp.tile([P, 512], F32, name="bt")
+                col = 16 + n0 // P + fb
+                nc.scalar.activation(out=bt[:], in_=acc[:], func=ACT.Silu, bias=pc[:, col : col + 1], scale=1.0)
+                tiles.append(bt)
+            bts[(n0, g)] = tiles
+
+        def turn_and_store(n0, g):
+            tiles = bts[(n0, g)]
+            for i in range(4):
+                tb = psum.tile([P, 512], F32, name="tb", tag="tb")
+                for fb in range(4):
+                    nc.tensor.transpose(out=tb[:, P * fb : P * fb + P], in_=tiles[fb][:, P * i : P * i + P], identity=ident_f[:])
+                ot = opool.tile([P, 512], F32, name="ot")
+                count[0] += 1
+                leave_psum("S" if count[0] % EV_S_EVERY == 0 else "V", ot[:], tb[:])
+                nc.sync.dma_start(out=uv[n0 // E][:, 4 * g + i, n0 % E : n0 % E + 512], in_=ot[:])
 
         def produce_z():
-            zt = opool.tile([P, MT, S], F32, name="zt", tag="ot")
+            outs = []
+            for w in range(2):
+                outs.append(const.tile([P, MT, S], F32, name="qk%d" % w))
             for g in range(2):
-                acc = psum.tile([P, 4, S], F32, name="accz", tag="ps")
-                for i in range(4):
-                    pr, mm = (4 * g + i) // 2, i % 2
-                    for c in range(2):
-                        nc.tensor.matmul_mx(
-                            out=acc[:, i, :],
-                            lhsT=xcodes[:, pr, c, P * mm : P * mm + P].bitcast(FP8X4),
-                            lhsT_scale=xscales[:, pr, c, P * mm : P * mm + P],
-                            rhs=zcodes[:, c, :].bitcast(FP8X4),
-                            rhs_scale=zscales[:, c, :],
-                            start=(c == 0),
-                            stop=(c == 1),
-                        )
-                nc.vector.tensor_tensor(
-                    out=zt[:, 4 * g : 4 * g + 4, :],
-                    in0=acc[:],
-                    in1=bias_bc[:, 2 * E : F].unsqueeze(1).to_broadcast([P, 4, S]),
-                    op=ALU.add,
-                )
-            nc.scalar.activation(out=zt[:], in_=zt[:], func=ACT.Silu)
-            for i in range(2):
-                gam = qk_bc[:, 2 * i, :].unsqueeze(1).to_broadcast([P, MT, S])
-                bet = qk_bc[:, 2 * i + 1, :].unsqueeze(1).to_broadcast([P, MT, S])
-                qt = opool.tile([P, MT, S], F32, name="qt", tag="ot")
-                nc.gpsimd.tensor_tensor(out=qt[:], in0=zt[:], in1=gam, op=ALU.mult)
-                nc.gpsimd.tensor_tensor(out=qt[:], in0=qt[:], in1=bet, op=ALU.add)
-                nc.sync.dma_start(out=qkv[i], in_=qt[:])
+                acc = psum.tile([P, 512], F32, name="accz", tag="acc")
+                for c in range(2):
+                    nc.tensor.matmul_mx(
+                        out=acc[:],
+                        lhsT=zcodes[:, c, :].bitcast(FP8X4),
+                        lhsT_scale=zscales[:, c, :],
+                        rhs=xcodes[:, g, c, :].bitcast(FP8X4),
+                        rhs_scale=xscales[:, g, c, :],
+                        start=(c == 0),
+                        stop=(c == 1),
+                    )
+                zt = btp.tile([P, 512], F32, name="zt", tag="bt")
+                nc.scalar.activation(out=zt[:], in_=acc[:], func=ACT.Silu, bias=pc[:, 48:49], scale=1.0)
+                for w in range(2):
+                    qt = btp.tile([P, 512], F32, name="qt", tag="bt")
+                    nc.gpsimd.tensor_scalar(
+                        out=qt[:],
+                        in0=zt[:],
+                        scalar1=pc[:, 49 + 2 * w : 50 + 2 * w],
+                        scalar2=pc[:, 50 + 2 * w : 51 + 2 * w],
+                        op0=ALU.mult,
+                        op1=ALU.add,
+                    )
+                    tb = psum.tile([P, 4, S], F32, name="tbz", tag="tb")
+                    for i in range(4):
+                        nc.tensor.transpose(out=tb[:, i, :], in_=qt[:, P * i : P * i + P], identity=ident_f[:])
+                    leave_psum("V", outs[w][:, 4 * g : 4 * g + 4, :], tb[:])
+            for w in range(2):
+                nc.sync.dma_start(out=qkv[w], in_=outs[w][:])
 
-        layer_norm(0)
+        units = []
+        for ch in range(NCH):
+            for h in range(2):
+                for g in range(2):
+                    units.append((CH * ch + 512 * h, g))
+        ln_stats(0)
         quantise_chunk(0)
-        layer_norm(1)
-        produce(0, 0)
-        produce(0, 1)
-        layer_norm(2)
-        produce(0, 2)
-        produce(0, 3)
-        layer_norm(3)
+        ln_stats(1)
+        ln_finish(0)
+        ln_finish(1)
         quantise_chunk(1)
-        for m in range(4, MT):
-            produce(0, m)
-        quantise_chunk(2)
-        for m in range(MT):
-            produce(1, m)
-        quantise_chunk(3)
-        quantise_z()
-        for m in range(MT):
-            produce(2, m)
-        produce_z()
-        for m in range(MT):
-            produce(3, m)
+        multiply(units[0][0], units[0][1])
+        for k in range(len(units)):
+            if k + 1 < len(units):
+                multiply(units[k + 1][0], units[k + 1][1])
+            turn_and_store(units[k][0], units[k][1])
+            if k == 1:
+                quantise_chunk(2)
+            if k == 5:
+                quantise_chunk(3)
+            if k == 8:
+                quantise_z()
+            if k == 11:
+                produce_z()

@@ -13,295 +13,248 @@ ALU = mybir.AluOpType
 ACT = mybir.ActivationFunctionType
 
 P = 128
+PACK = 4
+PASSES = 2
 ROWS = 1024
 D = 1024
 E = 2048
 S = 128
 F = E + E + S
-MT = ROWS // P
-CH = 1024
-NCH = (E + E) // CH
+ROW_TILES = ROWS // P
+PAIRS = ROW_TILES // 2
+K_TILES = D // P
+BANK = 512
+CHUNK = 1024
+CHUNKS = (E + E) // CHUNK
 LN_EPS = 1e-5
 FLOPS = 2 * ROWS * D * F
-
-BTBUFS = 8
-OBUFS = 8
-EV_S_EVERY = 6
-WENG = [["S", "S"], ["V", "V"], ["V", "V"], ["V", "V"]]
-NORM_ENG = ["G", "S", "G", "S", "G", "S", "G", "S"]
-XG_ENG = ["VV", "VV"]
 
 
 def tile_gaublock_pb_kernel(
     tc, x, ln_g, ln_b, W_in, b_in, gamma_q, beta_q, gamma_k, beta_k, out_0, out_1, out_2, out_3
 ):
     nc = tc.nc
-    xv = x.flatten_outer_dims().rearrange("(p m) k -> p m k", m=MT)
-    wv = W_in.rearrange("(j p) n -> p j n", p=P)
-    uv = [
-        out_0.flatten_outer_dims().rearrange("(p m) f -> p m f", m=MT),
-        out_1.flatten_outer_dims().rearrange("(p m) f -> p m f", m=MT),
-    ]
-    qkv = [
-        out_2.flatten_outer_dims().rearrange("(p m) s -> p m s", m=MT),
-        out_3.flatten_outer_dims().rearrange("(p m) s -> p m s", m=MT),
-    ]
+    x_rows = x.flatten_outer_dims().rearrange("(p m) k -> p m k", m=ROW_TILES)
+    w_rows = W_in.rearrange("(j p) n -> p j n", p=P)
+    uv_rows = [out.flatten_outer_dims().rearrange("(p m) f -> p m f", m=ROW_TILES) for out in (out_0, out_1)]
+    qk_rows = [out.flatten_outer_dims().rearrange("(p m) s -> p m s", m=ROW_TILES) for out in (out_2, out_3)]
 
     with ExitStack() as ctx:
-        const = ctx.enter_context(tc.tile_pool(name="const", bufs=1))
-        small = ctx.enter_context(tc.tile_pool(name="small", bufs=2))
-        ypool = ctx.enter_context(tc.tile_pool(name="ypool", bufs=4))
-        xstage = ctx.enter_context(tc.tile_pool(name="xstage", bufs=2))
-        wgrp = ctx.enter_context(tc.tile_pool(name="wgrp", bufs=2))
-        btp = ctx.enter_context(tc.tile_pool(name="btp", bufs=BTBUFS))
-        opool = ctx.enter_context(tc.tile_pool(name="opool", bufs=OBUFS))
-        psum = ctx.enter_context(tc.psum_pool(name="psum", bufs=4))
+        keep = ctx.enter_context(tc.tile_pool(name="keep", bufs=1))
+        stat = ctx.enter_context(tc.tile_pool(name="stat", bufs=2))
+        normed = ctx.enter_context(tc.tile_pool(name="normed", bufs=4))
+        stage = ctx.enter_context(tc.tile_pool(name="stage", bufs=2))
+        result = ctx.enter_context(tc.tile_pool(name="result", bufs=4))
+        psum = ctx.enter_context(tc.psum_pool(name="psum", bufs=8))
 
-        prm = const.tile([P, P], BF16, name="prm")
-        nc.vector.memset(prm[:].bitcast(I32), 0)
-        nc.scalar.dma_start(out=prm[0:8, :], in_=ln_g.rearrange("(j p) -> j p", p=P))
-        nc.scalar.dma_start(out=prm[8:16, :], in_=ln_b.rearrange("(j p) -> j p", p=P))
-        mhalf = const.tile([P, 4], F32, name="mhalf")
-        nc.vector.memset(mhalf[:], -0.5)
-        ident_f = const.tile([P, P], F32, name="ident_f")
-        make_identity(nc, ident_f[:])
-        ident_b = const.tile([P, P], BF16, name="ident_b")
-        nc.vector.tensor_copy(out=ident_b[:], in_=ident_f[:])
+        ln_rows = keep.tile([P, P], BF16, name="ln_rows")
+        nc.vector.memset(ln_rows[:].bitcast(I32), 0)
+        nc.scalar.dma_start(out=ln_rows[0:K_TILES, :], in_=ln_g.rearrange("(j p) -> j p", p=P))
+        nc.scalar.dma_start(out=ln_rows[K_TILES : 2 * K_TILES, :], in_=ln_b.rearrange("(j p) -> j p", p=P))
+        minus_half = keep.tile([P, 2], F32, name="minus_half")
+        nc.vector.memset(minus_half[:], -0.5)
+        ident_f32 = keep.tile([P, P], F32, name="ident_f32")
+        make_identity(nc, ident_f32[:])
+        ident_bf16 = keep.tile([P, P], BF16, name="ident_bf16")
+        nc.vector.tensor_copy(out=ident_bf16[:], in_=ident_f32[:])
 
-        xs = const.tile([P, MT, D], BF16, name="xs")
-        raws = {}
-        zraw = const.tile([P, 8, S], BF16, name="zraw")
+        x_sb = keep.tile([P, ROW_TILES, D], BF16, name="x_sb")
+        w_raw = {}
+        bias_all = keep.tile([P, F], BF16, name="bias_all")
+        qk_all = keep.tile([P, 4, S], BF16, name="qk_all")
+        wz_raw = keep.tile([P, K_TILES, S], BF16, name="wz_raw")
 
-        def load_x(i):
-            nc.sync.dma_start(out=xs[:, 2 * i : 2 * i + 2, :], in_=xv[:, 2 * i : 2 * i + 2, :])
+        def load_x(pair):
+            nc.sync.dma_start(out=x_sb[:, 2 * pair : 2 * pair + 2, :], in_=x_rows[:, 2 * pair : 2 * pair + 2, :])
 
-        def load_w(ch, c):
-            raw = const.tile([P, 4, CH], BF16, name="raw%d_%d" % (ch, c))
-            nc.sync.dma_start(out=raw[:], in_=wv[:, 4 * c : 4 * c + 4, CH * ch : CH * (ch + 1)])
-            raws[(ch, c)] = raw
+        def load_w(chunk):
+            for c in range(PASSES):
+                raw = keep.tile([P, PACK, CHUNK], BF16, name="w_raw%d_%d" % (chunk, c))
+                nc.sync.dma_start(
+                    out=raw[:], in_=w_rows[:, PACK * c : PACK * (c + 1), CHUNK * chunk : CHUNK * (chunk + 1)]
+                )
+                w_raw[(chunk, c)] = raw
 
         load_x(0)
         load_x(1)
-        load_w(0, 0)
-        load_w(0, 1)
+        load_w(0)
         load_x(2)
         load_x(3)
-        nc.scalar.dma_start(out=prm[16:49, :], in_=b_in.rearrange("(j p) -> j p", p=P))
-        for i, vec in enumerate([gamma_q, beta_q, gamma_k, beta_k]):
-            nc.scalar.dma_start(out=prm[49 + i : 50 + i, :], in_=vec.unsqueeze(0))
-        for ch in range(1, NCH):
-            load_w(ch, 0)
-            load_w(ch, 1)
-        nc.sync.dma_start(out=zraw[:], in_=wv[:, :, 2 * E : F])
+        nc.sync.dma_start(out=bias_all[:], in_=b_in.partition_broadcast(P))
+        for chunk in range(1, CHUNKS):
+            load_w(chunk)
+        nc.sync.dma_start(out=wz_raw[:], in_=w_rows[:, :, 2 * E : F])
+        for i, vec in enumerate((gamma_q, beta_q, gamma_k, beta_k)):
+            nc.sync.dma_start(out=qk_all[:, i, :], in_=vec.partition_broadcast(P))
 
-        pc_ps = psum.tile([P, P], F32, name="pc_ps", tag="tb")
-        nc.tensor.matmul(out=pc_ps[:], lhsT=prm[:], rhs=ident_b[:], start=True, stop=True)
-        pc = const.tile([P, 64], F32, name="pc")
-        nc.vector.tensor_copy(out=pc[:], in_=pc_ps[:, 0:64])
+        ln_ps = psum.tile([P, P], F32, name="ln_ps", tag="bank")
+        nc.tensor.matmul(out=ln_ps[:], lhsT=ln_rows[:], rhs=ident_bf16[:], start=True, stop=True)
+        ln_cols = keep.tile([P, 2 * K_TILES], F32, name="ln_cols")
+        nc.vector.tensor_copy(out=ln_cols[:], in_=ln_ps[:, 0 : 2 * K_TILES])
 
-        xcodes = const.tile([P, 2, 2, 512], U32, name="xcodes", align_bytes=64)
-        xscales = const.tile([P, 2, 2, 512], U8, name="xscales", align_bytes=64)
-        wcodes = const.tile([P, 2, 2 * E], U32, name="wcodes", align_bytes=64)
-        wscales = const.tile([P, 2, 2 * E], U8, name="wscales", align_bytes=64)
-        zcodes = const.tile([P, 2, S], U32, name="zcodes", align_bytes=64)
-        zscales = const.tile([P, 2, S], U8, name="zscales", align_bytes=64)
+        xn_codes = keep.tile([P, PAIRS, PASSES, 2 * P], U32, name="xn_codes", align_bytes=64)
+        xn_scales = keep.tile([P, PAIRS, PASSES, 2 * P], U8, name="xn_scales", align_bytes=64)
+        w_codes = keep.tile([P, PASSES, 2 * E], U32, name="w_codes", align_bytes=64)
+        w_scales = keep.tile([P, PASSES, 2 * E], U8, name="w_scales", align_bytes=64)
+        wz_codes = keep.tile([P, PASSES, S], U32, name="wz_codes", align_bytes=64)
+        wz_scales = keep.tile([P, PASSES, S], U8, name="wz_scales", align_bytes=64)
 
-        def regroup(eng, dst, src):
-            if eng == "G":
-                nc.gpsimd.tensor_scalar(
-                    out=dst, in0=src.rearrange("p t n -> p n t"), scalar1=1.0, scalar2=0.0, op0=ALU.mult, op1=ALU.add
-                )
-            else:
-                d4 = dst.rearrange("p (c i) t -> p c t i", i=4)
-                s4 = src.rearrange("p t (c i) -> p c t i", i=4)
-                if eng == "V":
-                    nc.vector.tensor_copy(out=d4, in_=s4)
-                else:
-                    nc.scalar.copy(out=d4, in_=s4)
+        def regroup(copy, dst, src):
+            copy(
+                out=dst.rearrange("p (a i) t -> p a t i", i=4),
+                in_=src.rearrange("p t (a i) -> p a t i", i=4),
+            )
 
-        def leave_psum(eng, dst, src):
-            if eng == "V":
-                nc.vector.tensor_copy(out=dst, in_=src)
-            else:
-                nc.scalar.copy(out=dst, in_=src)
-
-        ln_state = {}
-
-        def ln_stats(g):
-            stats = small.tile([P, 4, 2, 6], F32, name="stats")
-            mv = small.tile([P, 4, 2], F32, name="mv")
-            for i in range(4):
+        def layer_norm(pair):
+            stats = stat.tile([P, 2, 2, 6], F32, name="stats")
+            mean_var = stat.tile([P, 2, 2], F32, name="mean_var")
+            for i in range(2):
                 for h in range(2):
-                    nc.vector.bn_stats(out=stats[:, i, h, :], in_=xs[:, 4 * g + i, 512 * h : 512 * h + 512])
-                nc.vector.bn_aggr(out=mv[:, i, :], in_=stats[:, i, :, :].rearrange("p a b -> p (a b)"))
-            ve = small.tile([P, 4], F32, name="ve")
-            nc.gpsimd.tensor_scalar(out=ve[:], in0=mv[:, :, 1], scalar1=LN_EPS, scalar2=1.0, op0=ALU.add, op1=ALU.mult)
-            nmu = small.tile([P, 4], F32, name="nmu")
-            nc.gpsimd.tensor_scalar(out=nmu[:], in0=mv[:, :, 0], scalar1=-1.0, scalar2=0.0, op0=ALU.mult, op1=ALU.add)
-            rstd = small.tile([P, 4], F32, name="rstd")
-            nc.gpsimd.tensor_tensor(out=rstd[:], in0=ve[:], in1=mhalf[:], op=ALU.pow)
-            nmr = small.tile([P, 4], F32, name="nmr")
-            nc.gpsimd.tensor_tensor(out=nmr[:], in0=nmu[:], in1=rstd[:], op=ALU.mult)
-            ys = []
-            for i in range(4):
-                m = 4 * g + i
-                y = ypool.tile([P, D], F32, name="y")
-                if NORM_ENG[m] == "G":
-                    nc.gpsimd.tensor_scalar(
-                        out=y[:],
-                        in0=xs[:, m, :],
-                        scalar1=nmu[:, i : i + 1],
-                        scalar2=rstd[:, i : i + 1],
-                        op0=ALU.add,
-                        op1=ALU.mult,
-                    )
-                else:
-                    nc.scalar.activation(
-                        out=y[:], in_=xs[:, m, :], func=ACT.Identity, scale=rstd[:, i : i + 1], bias=nmr[:, i : i + 1]
-                    )
-                ys.append(y)
-            ln_state[g] = ys
-
-        def ln_finish(g):
-            ys = ln_state[g]
-            xg = xstage.tile([P, 2, 512, 4], BF16, name="xg", align_bytes=64, bufs=1)
-            for c in range(2):
-                planes = xstage.tile([P, 4, 512], BF16, name="planes")
-                xts = []
-                for t in range(4):
-                    xts.append(psum.tile([P, 512], F32, name="xt", tag="tb"))
-                for i in range(4):
-                    for t in range(4):
-                        j = 4 * c + t
+                    nc.vector.bn_stats(out=stats[:, i, h, :], in_=x_sb[:, 2 * pair + i, 512 * h : 512 * (h + 1)])
+                nc.vector.bn_aggr(out=mean_var[:, i, :], in_=stats[:, i, :, :].rearrange("p a b -> p (a b)"))
+            var_eps = stat.tile([P, 2], F32, name="var_eps")
+            nc.vector.tensor_scalar_add(out=var_eps[:], in0=mean_var[:, :, 1], scalar1=LN_EPS)
+            neg_mean = stat.tile([P, 2], F32, name="neg_mean")
+            nc.vector.tensor_scalar_mul(out=neg_mean[:], in0=mean_var[:, :, 0], scalar1=-1.0)
+            rstd = stat.tile([P, 2], F32, name="rstd")
+            nc.gpsimd.tensor_tensor(out=rstd[:], in0=var_eps[:], in1=minus_half[:], op=ALU.pow)
+            rows = []
+            for i in range(2):
+                y = normed.tile([P, D], F32, name="y")
+                nc.gpsimd.tensor_scalar(
+                    out=y[:],
+                    in0=x_sb[:, 2 * pair + i, :],
+                    scalar1=neg_mean[:, i : i + 1],
+                    scalar2=rstd[:, i : i + 1],
+                    op0=ALU.add,
+                    op1=ALU.mult,
+                )
+                rows.append(y)
+            k_tiles = stage.tile([P, K_TILES, 2 * P], BF16, name="k_tiles")
+            for a in range(K_TILES // 2):
+                turned = psum.tile([P, 2, 2 * P], F32, name="turned", tag="bank")
+                for b in range(2):
+                    j = 2 * a + b
+                    for i in range(2):
                         nc.tensor.transpose(
-                            out=xts[t][:, P * i : P * i + P], in_=ys[i][:, P * j : P * j + P], identity=ident_f[:]
+                            out=turned[:, b, P * i : P * (i + 1)], in_=rows[i][:, P * j : P * (j + 1)], identity=ident_f32[:]
                         )
-                for t in range(4):
-                    j = 4 * c + t
+                for b in range(2):
+                    j = 2 * a + b
                     nc.scalar.activation(
-                        out=planes[:, t, :], in_=xts[t][:], func=ACT.Identity, scale=pc[:, j : j + 1], bias=pc[:, 8 + j : 9 + j]
+                        out=k_tiles[:, j, :],
+                        in_=turned[:, b, :],
+                        func=ACT.Identity,
+                        scale=ln_cols[:, j : j + 1],
+                        bias=ln_cols[:, K_TILES + j : K_TILES + j + 1],
                     )
-                regroup(XG_ENG[g][c], xg[:, c, :, :], planes[:])
+            grouped = stage.tile([P, PASSES, 2 * P, PACK], BF16, name="xn_grouped", align_bytes=64)
+            for c in range(PASSES):
+                regroup(nc.scalar.copy, grouped[:, c, :, :], k_tiles[:, PACK * c : PACK * (c + 1), :])
             nc.vector.quantize_mx(
-                out=xcodes[:, g, :, :].rearrange("p c r -> p (c r)").bitcast(FP8X4),
-                scales=xscales[:, g, :, :].rearrange("p c r -> p (c r)"),
-                in_=xg[:].rearrange("p c r t -> p (c r t)"),
+                out=xn_codes[:, pair, :, :].rearrange("p c r -> p (c r)").bitcast(FP8X4),
+                scales=xn_scales[:, pair, :, :].rearrange("p c r -> p (c r)"),
+                in_=grouped[:].rearrange("p c r t -> p (c r t)"),
             )
 
-        def quantise_z():
-            zg = const.tile([P, 2, S, 4], BF16, name="zg", align_bytes=64)
-            for c in range(2):
-                regroup("V", zg[:, c, :, :], zraw[:, 4 * c : 4 * c + 4, :])
-            nc.vector.quantize_mx(
-                out=zcodes[:].rearrange("p c r -> p (c r)").bitcast(FP8X4),
-                scales=zscales[:].rearrange("p c r -> p (c r)"),
-                in_=zg[:].rearrange("p c r t -> p (c r t)"),
-            )
-
-        def quantise_chunk(ch):
-            for c in range(2):
-                raw = raws[(ch, c)]
-                wg = wgrp.tile([P, CH, 4], BF16, name="wg", align_bytes=64)
-                engs = WENG[ch][c]
-                w = CH // len(engs)
-                for h, eng in enumerate(engs):
-                    regroup(eng, wg[:, w * h : w * (h + 1), :], raw[:, :, w * h : w * (h + 1)])
+        def quantise_w(chunk):
+            cols = slice(CHUNK * chunk, CHUNK * (chunk + 1))
+            grouped = []
+            for c, copy in enumerate((nc.vector.tensor_copy, nc.scalar.copy)):
+                g = stage.tile([P, CHUNK, PACK], BF16, name="w_grouped", align_bytes=64)
+                regroup(copy, g[:], w_raw[(chunk, c)][:])
+                grouped.append(g)
+            for c in range(PASSES):
                 nc.vector.quantize_mx(
-                    out=wcodes[:, c, CH * ch : CH * (ch + 1)].bitcast(FP8X4),
-                    scales=wscales[:, c, CH * ch : CH * (ch + 1)],
-                    in_=wg[:].rearrange("p n t -> p (n t)"),
+                    out=w_codes[:, c, cols].bitcast(FP8X4),
+                    scales=w_scales[:, c, cols],
+                    in_=grouped[c][:].rearrange("p n t -> p (n t)"),
                 )
 
-        bts = {}
-        count = [0]
+        def quantise_wz():
+            grouped = keep.tile([P, PASSES, S, PACK], BF16, name="wz_grouped", align_bytes=64)
+            for c in range(PASSES):
+                regroup(nc.scalar.copy, grouped[:, c, :, :], wz_raw[:, PACK * c : PACK * (c + 1), :])
+            nc.vector.quantize_mx(
+                out=wz_codes[:].rearrange("p c n -> p (c n)").bitcast(FP8X4),
+                scales=wz_scales[:].rearrange("p c n -> p (c n)"),
+                in_=grouped[:].rearrange("p c n t -> p (c n t)"),
+            )
 
-        def multiply(n0, g):
-            tiles = []
-            for fb in range(4):
-                acc = psum.tile([P, 512], F32, name="acc", tag="acc")
-                for c in range(2):
-                    nc.tensor.matmul_mx(
-                        out=acc[:],
-                        lhsT=wcodes[:, c, n0 + P * fb : n0 + P * fb + P].bitcast(FP8X4),
-                        lhsT_scale=wscales[:, c, n0 + P * fb : n0 + P * fb + P],
-                        rhs=xcodes[:, g, c, :].bitcast(FP8X4),
-                        rhs_scale=xscales[:, g, c, :],
-                        start=(c == 0),
-                        stop=(c == 1),
+        def mx_group(acc, tile_m, rhs_codes, rhs_scales):
+            pair, i = tile_m // 2, tile_m % 2
+            for c in range(PASSES):
+                nc.tensor.matmul_mx(
+                    out=acc,
+                    lhsT=xn_codes[:, pair, c, P * i : P * (i + 1)].bitcast(FP8X4),
+                    lhsT_scale=xn_scales[:, pair, c, P * i : P * (i + 1)],
+                    rhs=rhs_codes[c].bitcast(FP8X4),
+                    rhs_scale=rhs_scales[c],
+                    start=(c == 0),
+                    stop=(c == PASSES - 1),
+                )
+
+        def project(chunk, pair):
+            out_sb = result.tile([P, 2, CHUNK], F32, name="out_sb")
+            for i in range(2):
+                for h in range(CHUNK // BANK):
+                    cols = slice(CHUNK * chunk + BANK * h, CHUNK * chunk + BANK * (h + 1))
+                    acc = psum.tile([P, BANK], F32, name="acc", tag="bank")
+                    mx_group(
+                        acc[:],
+                        2 * pair + i,
+                        [w_codes[:, c, cols] for c in range(PASSES)],
+                        [w_scales[:, c, cols] for c in range(PASSES)],
                     )
-                bt = btp.tile([P, 512], F32, name="bt")
-                col = 16 + n0 // P + fb
-                nc.scalar.activation(out=bt[:], in_=acc[:], func=ACT.Silu, bias=pc[:, col : col + 1], scale=1.0)
-                tiles.append(bt)
-            bts[(n0, g)] = tiles
+                    nc.vector.tensor_tensor(
+                        out=out_sb[:, i, BANK * h : BANK * (h + 1)], in0=acc[:], in1=bias_all[:, cols], op=ALU.add
+                    )
+            nc.scalar.activation(out=out_sb[:], in_=out_sb[:], func=ACT.Silu)
+            first = (CHUNK * chunk) % E
+            nc.sync.dma_start(
+                out=uv_rows[(CHUNK * chunk) // E][:, 2 * pair : 2 * pair + 2, first : first + CHUNK], in_=out_sb[:]
+            )
 
-        def turn_and_store(n0, g):
-            tiles = bts[(n0, g)]
-            for i in range(4):
-                tb = psum.tile([P, 512], F32, name="tb", tag="tb")
-                for fb in range(4):
-                    nc.tensor.transpose(out=tb[:, P * fb : P * fb + P], in_=tiles[fb][:, P * i : P * i + P], identity=ident_f[:])
-                ot = opool.tile([P, 512], F32, name="ot")
-                count[0] += 1
-                leave_psum("S" if count[0] % EV_S_EVERY == 0 else "V", ot[:], tb[:])
-                nc.sync.dma_start(out=uv[n0 // E][:, 4 * g + i, n0 % E : n0 % E + 512], in_=ot[:])
-
-        def produce_z():
-            outs = []
+        def project_z():
+            z_sb = result.tile([P, ROW_TILES, S], F32, name="z_sb", tag="out_sb")
+            per_bank = BANK // S
+            for a in range(ROW_TILES // per_bank):
+                acc = psum.tile([P, per_bank, S], F32, name="acc_z", tag="bank")
+                for i in range(per_bank):
+                    mx_group(
+                        acc[:, i, :],
+                        per_bank * a + i,
+                        [wz_codes[:, c, :] for c in range(PASSES)],
+                        [wz_scales[:, c, :] for c in range(PASSES)],
+                    )
+                nc.vector.tensor_tensor(
+                    out=z_sb[:, per_bank * a : per_bank * (a + 1), :],
+                    in0=acc[:],
+                    in1=bias_all[:, 2 * E : F].unsqueeze(1).to_broadcast([P, per_bank, S]),
+                    op=ALU.add,
+                )
+            nc.scalar.activation(out=z_sb[:], in_=z_sb[:], func=ACT.Silu)
             for w in range(2):
-                outs.append(const.tile([P, MT, S], F32, name="qk%d" % w))
-            for g in range(2):
-                acc = psum.tile([P, 512], F32, name="accz", tag="acc")
-                for c in range(2):
-                    nc.tensor.matmul_mx(
-                        out=acc[:],
-                        lhsT=zcodes[:, c, :].bitcast(FP8X4),
-                        lhsT_scale=zscales[:, c, :],
-                        rhs=xcodes[:, g, c, :].bitcast(FP8X4),
-                        rhs_scale=xscales[:, g, c, :],
-                        start=(c == 0),
-                        stop=(c == 1),
-                    )
-                zt = btp.tile([P, 512], F32, name="zt", tag="bt")
-                nc.scalar.activation(out=zt[:], in_=acc[:], func=ACT.Silu, bias=pc[:, 48:49], scale=1.0)
-                for w in range(2):
-                    qt = btp.tile([P, 512], F32, name="qt", tag="bt")
-                    nc.gpsimd.tensor_scalar(
-                        out=qt[:],
-                        in0=zt[:],
-                        scalar1=pc[:, 49 + 2 * w : 50 + 2 * w],
-                        scalar2=pc[:, 50 + 2 * w : 51 + 2 * w],
-                        op0=ALU.mult,
-                        op1=ALU.add,
-                    )
-                    tb = psum.tile([P, 4, S], F32, name="tbz", tag="tb")
-                    for i in range(4):
-                        nc.tensor.transpose(out=tb[:, i, :], in_=qt[:, P * i : P * i + P], identity=ident_f[:])
-                    leave_psum("V", outs[w][:, 4 * g : 4 * g + 4, :], tb[:])
-            for w in range(2):
-                nc.sync.dma_start(out=qkv[w], in_=outs[w][:])
+                gain = qk_all[:, 2 * w, :].unsqueeze(1).to_broadcast([P, ROW_TILES, S])
+                offset = qk_all[:, 2 * w + 1, :].unsqueeze(1).to_broadcast([P, ROW_TILES, S])
+                mapped = result.tile([P, ROW_TILES, S], F32, name="mapped", tag="out_sb")
+                nc.gpsimd.tensor_tensor(out=mapped[:], in0=z_sb[:], in1=gain, op=ALU.mult)
+                nc.gpsimd.tensor_tensor(out=mapped[:], in0=mapped[:], in1=offset, op=ALU.add)
+                nc.sync.dma_start(out=qk_rows[w], in_=mapped[:])
 
-        units = []
-        for ch in range(NCH):
-            for h in range(2):
-                for g in range(2):
-                    units.append((CH * ch + 512 * h, g))
-        ln_stats(0)
-        quantise_chunk(0)
-        ln_stats(1)
-        ln_finish(0)
-        ln_finish(1)
-        quantise_chunk(1)
-        multiply(units[0][0], units[0][1])
-        for k in range(len(units)):
-            if k + 1 < len(units):
-                multiply(units[k + 1][0], units[k + 1][1])
-            turn_and_store(units[k][0], units[k][1])
-            if k == 1:
-                quantise_chunk(2)
-            if k == 5:
-                quantise_chunk(3)
-            if k == 8:
-                quantise_z()
-            if k == 11:
-                produce_z()
+        layer_norm(0)
+        quantise_w(0)
+        for pair in range(PAIRS):
+            if pair + 1 < PAIRS:
+                layer_norm(pair + 1)
+            else:
+                quantise_w(1)
+            project(0, pair)
+        for chunk in range(1, CHUNKS):
+            if chunk + 1 < CHUNKS:
+                quantise_w(chunk + 1)
+            else:
+                quantise_wz()
+                project_z()
+            for pair in range(PAIRS):
+                project(chunk, pair)

@@ -26,6 +26,7 @@ K_TILES = D // P
 BANK = 512
 CHUNK = 1024
 CHUNKS = (E + E) // CHUNK
+GPSIMD_PIECES = 4
 LN_EPS = 1e-5
 FLOPS = 2 * ROWS * D * F
 
@@ -105,6 +106,11 @@ def tile_gaublock_pb_kernel(
                 in_=src.rearrange("p t (a i) -> p a t i", i=4),
             )
 
+        def regroup_on_gpsimd(dst, src):
+            nc.gpsimd.tensor_scalar(
+                out=dst, in0=src.rearrange("p t n -> p n t"), scalar1=1.0, scalar2=0.0, op0=ALU.mult, op1=ALU.add
+            )
+
         def layer_norm(pair):
             stats = stat.tile([P, 2, 2, 6], F32, name="stats")
             mean_var = stat.tile([P, 2, 2], F32, name="mean_var")
@@ -113,23 +119,31 @@ def tile_gaublock_pb_kernel(
                     nc.vector.bn_stats(out=stats[:, i, h, :], in_=x_sb[:, 2 * pair + i, 512 * h : 512 * (h + 1)])
                 nc.vector.bn_aggr(out=mean_var[:, i, :], in_=stats[:, i, :, :].rearrange("p a b -> p (a b)"))
             var_eps = stat.tile([P, 2], F32, name="var_eps")
-            nc.vector.tensor_scalar_add(out=var_eps[:], in0=mean_var[:, :, 1], scalar1=LN_EPS)
+            nc.gpsimd.tensor_scalar(
+                out=var_eps[:], in0=mean_var[:, :, 1], scalar1=LN_EPS, scalar2=1.0, op0=ALU.add, op1=ALU.mult
+            )
             neg_mean = stat.tile([P, 2], F32, name="neg_mean")
-            nc.vector.tensor_scalar_mul(out=neg_mean[:], in0=mean_var[:, :, 0], scalar1=-1.0)
+            nc.gpsimd.tensor_scalar(
+                out=neg_mean[:], in0=mean_var[:, :, 0], scalar1=-1.0, scalar2=0.0, op0=ALU.mult, op1=ALU.add
+            )
             rstd = stat.tile([P, 2], F32, name="rstd")
             nc.gpsimd.tensor_tensor(out=rstd[:], in0=var_eps[:], in1=minus_half[:], op=ALU.pow)
-            rows = []
-            for i in range(2):
-                y = normed.tile([P, D], F32, name="y")
-                nc.gpsimd.tensor_scalar(
-                    out=y[:],
-                    in0=x_sb[:, 2 * pair + i, :],
-                    scalar1=neg_mean[:, i : i + 1],
-                    scalar2=rstd[:, i : i + 1],
-                    op0=ALU.add,
-                    op1=ALU.mult,
-                )
-                rows.append(y)
+            shift = stat.tile([P, 2], F32, name="shift")
+            nc.gpsimd.tensor_tensor(out=shift[:], in0=neg_mean[:], in1=rstd[:], op=ALU.mult)
+            y_first = normed.tile([P, D], F32, name="y")
+            nc.gpsimd.tensor_scalar(
+                out=y_first[:],
+                in0=x_sb[:, 2 * pair, :],
+                scalar1=neg_mean[:, 0:1],
+                scalar2=rstd[:, 0:1],
+                op0=ALU.add,
+                op1=ALU.mult,
+            )
+            y_second = normed.tile([P, D], F32, name="y")
+            nc.scalar.activation(
+                out=y_second[:], in_=x_sb[:, 2 * pair + 1, :], func=ACT.Identity, scale=rstd[:, 1:2], bias=shift[:, 1:2]
+            )
+            rows = [y_first, y_second]
             k_tiles = stage.tile([P, K_TILES, 2 * P], BF16, name="k_tiles")
             for a in range(K_TILES // 2):
                 turned = psum.tile([P, 2, 2 * P], F32, name="turned", tag="bank")
@@ -150,7 +164,7 @@ def tile_gaublock_pb_kernel(
                     )
             grouped = stage.tile([P, PASSES, 2 * P, PACK], BF16, name="xn_grouped", align_bytes=64)
             for c in range(PASSES):
-                regroup(nc.scalar.copy, grouped[:, c, :, :], k_tiles[:, PACK * c : PACK * (c + 1), :])
+                regroup(nc.vector.tensor_copy, grouped[:, c, :, :], k_tiles[:, PACK * c : PACK * (c + 1), :])
             nc.vector.quantize_mx(
                 out=xn_codes[:, pair, :, :].rearrange("p c r -> p (c r)").bitcast(FP8X4),
                 scales=xn_scales[:, pair, :, :].rearrange("p c r -> p (c r)"),
@@ -160,10 +174,16 @@ def tile_gaublock_pb_kernel(
         def quantise_w(chunk):
             cols = slice(CHUNK * chunk, CHUNK * (chunk + 1))
             grouped = []
-            for c, copy in enumerate((nc.vector.tensor_copy, nc.scalar.copy)):
-                g = stage.tile([P, CHUNK, PACK], BF16, name="w_grouped", align_bytes=64)
-                regroup(copy, g[:], w_raw[(chunk, c)][:])
-                grouped.append(g)
+            for c in range(PASSES):
+                grouped.append(stage.tile([P, CHUNK, PACK], BF16, name="w_grouped", align_bytes=64))
+            regroup(nc.scalar.copy, grouped[0][:], w_raw[(chunk, 0)][:])
+            if chunk == 0:
+                regroup(nc.scalar.copy, grouped[1][:], w_raw[(chunk, 1)][:])
+            else:
+                width = CHUNK // GPSIMD_PIECES
+                for a in range(GPSIMD_PIECES):
+                    piece = slice(width * a, width * (a + 1))
+                    regroup_on_gpsimd(grouped[1][:, piece, :], w_raw[(chunk, 1)][:, :, piece])
             for c in range(PASSES):
                 nc.vector.quantize_mx(
                     out=w_codes[:, c, cols].bitcast(FP8X4),

@@ -26,7 +26,6 @@ K_TILES = D // P
 BANK = 512
 CHUNK = 1024
 CHUNKS = (E + E) // CHUNK
-GPSIMD_PIECES = 4
 LN_EPS = 1e-5
 FLOPS = 2 * ROWS * D * F
 
@@ -45,7 +44,8 @@ def tile_gaublock_pb_kernel(
         stat = ctx.enter_context(tc.tile_pool(name="stat", bufs=2))
         normed = ctx.enter_context(tc.tile_pool(name="normed", bufs=4))
         stage = ctx.enter_context(tc.tile_pool(name="stage", bufs=2))
-        result = ctx.enter_context(tc.tile_pool(name="result", bufs=4))
+        weights = ctx.enter_context(tc.tile_pool(name="weights", bufs=4))
+        result = ctx.enter_context(tc.tile_pool(name="result", bufs=8))
         psum = ctx.enter_context(tc.psum_pool(name="psum", bufs=8))
 
         ln_rows = keep.tile([P, P], BF16, name="ln_rows")
@@ -70,7 +70,7 @@ def tile_gaublock_pb_kernel(
 
         def load_w(chunk):
             for c in range(PASSES):
-                raw = keep.tile([P, PACK, CHUNK], BF16, name="w_raw%d_%d" % (chunk, c))
+                raw = weights.tile([P, PACK, CHUNK], BF16, name="w_raw")
                 nc.sync.dma_start(
                     out=raw[:], in_=w_rows[:, PACK * c : PACK * (c + 1), CHUNK * chunk : CHUNK * (chunk + 1)]
                 )
@@ -82,8 +82,7 @@ def tile_gaublock_pb_kernel(
         load_x(2)
         load_x(3)
         nc.sync.dma_start(out=bias_all[:], in_=b_in.partition_broadcast(P))
-        for chunk in range(1, CHUNKS):
-            load_w(chunk)
+        load_w(1)
         nc.sync.dma_start(out=wz_raw[:], in_=w_rows[:, :, 2 * E : F])
         for i, vec in enumerate((gamma_q, beta_q, gamma_k, beta_k)):
             nc.sync.dma_start(out=qk_all[:, i, :], in_=vec.partition_broadcast(P))
@@ -106,11 +105,6 @@ def tile_gaublock_pb_kernel(
                 in_=src.rearrange("p t (a i) -> p a t i", i=4),
             )
 
-        def regroup_on_gpsimd(dst, src):
-            nc.gpsimd.tensor_scalar(
-                out=dst, in0=src.rearrange("p t n -> p n t"), scalar1=1.0, scalar2=0.0, op0=ALU.mult, op1=ALU.add
-            )
-
         def layer_norm(pair):
             stats = stat.tile([P, 2, 2, 6], F32, name="stats")
             mean_var = stat.tile([P, 2, 2], F32, name="mean_var")
@@ -119,31 +113,23 @@ def tile_gaublock_pb_kernel(
                     nc.vector.bn_stats(out=stats[:, i, h, :], in_=x_sb[:, 2 * pair + i, 512 * h : 512 * (h + 1)])
                 nc.vector.bn_aggr(out=mean_var[:, i, :], in_=stats[:, i, :, :].rearrange("p a b -> p (a b)"))
             var_eps = stat.tile([P, 2], F32, name="var_eps")
-            nc.gpsimd.tensor_scalar(
-                out=var_eps[:], in0=mean_var[:, :, 1], scalar1=LN_EPS, scalar2=1.0, op0=ALU.add, op1=ALU.mult
-            )
+            nc.vector.tensor_scalar_add(out=var_eps[:], in0=mean_var[:, :, 1], scalar1=LN_EPS)
             neg_mean = stat.tile([P, 2], F32, name="neg_mean")
-            nc.gpsimd.tensor_scalar(
-                out=neg_mean[:], in0=mean_var[:, :, 0], scalar1=-1.0, scalar2=0.0, op0=ALU.mult, op1=ALU.add
-            )
+            nc.vector.tensor_scalar_mul(out=neg_mean[:], in0=mean_var[:, :, 0], scalar1=-1.0)
             rstd = stat.tile([P, 2], F32, name="rstd")
             nc.gpsimd.tensor_tensor(out=rstd[:], in0=var_eps[:], in1=minus_half[:], op=ALU.pow)
-            shift = stat.tile([P, 2], F32, name="shift")
-            nc.gpsimd.tensor_tensor(out=shift[:], in0=neg_mean[:], in1=rstd[:], op=ALU.mult)
-            y_first = normed.tile([P, D], F32, name="y")
-            nc.gpsimd.tensor_scalar(
-                out=y_first[:],
-                in0=x_sb[:, 2 * pair, :],
-                scalar1=neg_mean[:, 0:1],
-                scalar2=rstd[:, 0:1],
-                op0=ALU.add,
-                op1=ALU.mult,
-            )
-            y_second = normed.tile([P, D], F32, name="y")
-            nc.scalar.activation(
-                out=y_second[:], in_=x_sb[:, 2 * pair + 1, :], func=ACT.Identity, scale=rstd[:, 1:2], bias=shift[:, 1:2]
-            )
-            rows = [y_first, y_second]
+            rows = []
+            for i in range(2):
+                y = normed.tile([P, D], F32, name="y")
+                nc.gpsimd.tensor_scalar(
+                    out=y[:],
+                    in0=x_sb[:, 2 * pair + i, :],
+                    scalar1=neg_mean[:, i : i + 1],
+                    scalar2=rstd[:, i : i + 1],
+                    op0=ALU.add,
+                    op1=ALU.mult,
+                )
+                rows.append(y)
             k_tiles = stage.tile([P, K_TILES, 2 * P], BF16, name="k_tiles")
             for a in range(K_TILES // 2):
                 turned = psum.tile([P, 2, 2 * P], F32, name="turned", tag="bank")
@@ -164,7 +150,7 @@ def tile_gaublock_pb_kernel(
                     )
             grouped = stage.tile([P, PASSES, 2 * P, PACK], BF16, name="xn_grouped", align_bytes=64)
             for c in range(PASSES):
-                regroup(nc.vector.tensor_copy, grouped[:, c, :, :], k_tiles[:, PACK * c : PACK * (c + 1), :])
+                regroup(nc.scalar.copy, grouped[:, c, :, :], k_tiles[:, PACK * c : PACK * (c + 1), :])
             nc.vector.quantize_mx(
                 out=xn_codes[:, pair, :, :].rearrange("p c r -> p (c r)").bitcast(FP8X4),
                 scales=xn_scales[:, pair, :, :].rearrange("p c r -> p (c r)"),
@@ -174,16 +160,10 @@ def tile_gaublock_pb_kernel(
         def quantise_w(chunk):
             cols = slice(CHUNK * chunk, CHUNK * (chunk + 1))
             grouped = []
-            for c in range(PASSES):
-                grouped.append(stage.tile([P, CHUNK, PACK], BF16, name="w_grouped", align_bytes=64))
-            regroup(nc.scalar.copy, grouped[0][:], w_raw[(chunk, 0)][:])
-            if chunk == 0:
-                regroup(nc.scalar.copy, grouped[1][:], w_raw[(chunk, 1)][:])
-            else:
-                width = CHUNK // GPSIMD_PIECES
-                for a in range(GPSIMD_PIECES):
-                    piece = slice(width * a, width * (a + 1))
-                    regroup_on_gpsimd(grouped[1][:, piece, :], w_raw[(chunk, 1)][:, :, piece])
+            for c, copy in enumerate((nc.vector.tensor_copy, nc.scalar.copy)):
+                g = stage.tile([P, CHUNK, PACK], BF16, name="w_grouped", align_bytes=64)
+                regroup(copy, g[:], w_raw[(chunk, c)][:])
+                grouped.append(g)
             for c in range(PASSES):
                 nc.vector.quantize_mx(
                     out=w_codes[:, c, cols].bitcast(FP8X4),
@@ -264,11 +244,13 @@ def tile_gaublock_pb_kernel(
 
         layer_norm(0)
         quantise_w(0)
+        load_w(2)
         for pair in range(PAIRS):
             if pair + 1 < PAIRS:
                 layer_norm(pair + 1)
             else:
                 quantise_w(1)
+                load_w(3)
             project(0, pair)
         for chunk in range(1, CHUNKS):
             if chunk + 1 < CHUNKS:

@@ -34,18 +34,17 @@ def tile_gaublock_pb_kernel(
     tc, x, ln_g, ln_b, W_in, b_in, gamma_q, beta_q, gamma_k, beta_k, out_0, out_1, out_2, out_3
 ):
     nc = tc.nc
-    x_rows = x.flatten_outer_dims().rearrange("(p m) k -> p m k", m=ROW_TILES)
+    x_rows = x.flatten_outer_dims().rearrange("(m p) k -> p m k", p=P)
     w_rows = W_in.rearrange("(j p) n -> p j n", p=P)
-    uv_rows = [out.flatten_outer_dims().rearrange("(p m) f -> p m f", m=ROW_TILES) for out in (out_0, out_1)]
-    qk_rows = [out.flatten_outer_dims().rearrange("(p m) s -> p m s", m=ROW_TILES) for out in (out_2, out_3)]
+    uv_rows = [out.flatten_outer_dims().rearrange("(m p) f -> p m f", p=P) for out in (out_0, out_1)]
+    qk_rows = [out.flatten_outer_dims().rearrange("(m p) s -> p m s", p=P) for out in (out_2, out_3)]
 
     with ExitStack() as ctx:
         keep = ctx.enter_context(tc.tile_pool(name="keep", bufs=1))
         stat = ctx.enter_context(tc.tile_pool(name="stat", bufs=2))
         normed = ctx.enter_context(tc.tile_pool(name="normed", bufs=4))
         stage = ctx.enter_context(tc.tile_pool(name="stage", bufs=2))
-        weights = ctx.enter_context(tc.tile_pool(name="weights", bufs=4))
-        result = ctx.enter_context(tc.tile_pool(name="result", bufs=8))
+        result = ctx.enter_context(tc.tile_pool(name="result", bufs=4))
         psum = ctx.enter_context(tc.psum_pool(name="psum", bufs=8))
 
         ln_rows = keep.tile([P, P], BF16, name="ln_rows")
@@ -70,7 +69,7 @@ def tile_gaublock_pb_kernel(
 
         def load_w(chunk):
             for c in range(PASSES):
-                raw = weights.tile([P, PACK, CHUNK], BF16, name="w_raw")
+                raw = keep.tile([P, PACK, CHUNK], BF16, name="w_raw%d_%d" % (chunk, c))
                 nc.sync.dma_start(
                     out=raw[:], in_=w_rows[:, PACK * c : PACK * (c + 1), CHUNK * chunk : CHUNK * (chunk + 1)]
                 )
@@ -82,7 +81,8 @@ def tile_gaublock_pb_kernel(
         load_x(2)
         load_x(3)
         nc.sync.dma_start(out=bias_all[:], in_=b_in.partition_broadcast(P))
-        load_w(1)
+        for chunk in range(1, CHUNKS):
+            load_w(chunk)
         nc.sync.dma_start(out=wz_raw[:], in_=w_rows[:, :, 2 * E : F])
         for i, vec in enumerate((gamma_q, beta_q, gamma_k, beta_k)):
             nc.sync.dma_start(out=qk_all[:, i, :], in_=vec.partition_broadcast(P))
@@ -244,13 +244,11 @@ def tile_gaublock_pb_kernel(
 
         layer_norm(0)
         quantise_w(0)
-        load_w(2)
         for pair in range(PAIRS):
             if pair + 1 < PAIRS:
                 layer_norm(pair + 1)
             else:
                 quantise_w(1)
-                load_w(3)
             project(0, pair)
         for chunk in range(1, CHUNKS):
             if chunk + 1 < CHUNKS:

@@ -22,6 +22,8 @@ S = 128
 F = E + E + S
 ROW_TILES = ROWS // P
 PAIRS = ROW_TILES // 2
+GROUP = 4
+GROUPS = ROW_TILES // GROUP
 K_TILES = D // P
 BANK = 512
 CHUNK = 1024
@@ -34,15 +36,15 @@ def tile_gaublock_pb_kernel(
     tc, x, ln_g, ln_b, W_in, b_in, gamma_q, beta_q, gamma_k, beta_k, out_0, out_1, out_2, out_3
 ):
     nc = tc.nc
-    x_rows = x.flatten_outer_dims().rearrange("(m p) k -> p m k", p=P)
+    x_rows = x.flatten_outer_dims().rearrange("(p m) k -> p m k", m=ROW_TILES)
     w_rows = W_in.rearrange("(j p) n -> p j n", p=P)
-    uv_rows = [out.flatten_outer_dims().rearrange("(m p) f -> p m f", p=P) for out in (out_0, out_1)]
-    qk_rows = [out.flatten_outer_dims().rearrange("(m p) s -> p m s", p=P) for out in (out_2, out_3)]
+    uv_rows = [out.flatten_outer_dims().rearrange("(p m) f -> p m f", m=ROW_TILES) for out in (out_0, out_1)]
+    qk_rows = [out.flatten_outer_dims().rearrange("(p m) s -> p m s", m=ROW_TILES) for out in (out_2, out_3)]
 
     with ExitStack() as ctx:
         keep = ctx.enter_context(tc.tile_pool(name="keep", bufs=1))
         stat = ctx.enter_context(tc.tile_pool(name="stat", bufs=2))
-        normed = ctx.enter_context(tc.tile_pool(name="normed", bufs=4))
+        normed = ctx.enter_context(tc.tile_pool(name="normed", bufs=GROUP))
         stage = ctx.enter_context(tc.tile_pool(name="stage", bufs=2))
         result = ctx.enter_context(tc.tile_pool(name="result", bufs=4))
         psum = ctx.enter_context(tc.psum_pool(name="psum", bufs=8))
@@ -51,7 +53,7 @@ def tile_gaublock_pb_kernel(
         nc.vector.memset(ln_rows[:].bitcast(I32), 0)
         nc.scalar.dma_start(out=ln_rows[0:K_TILES, :], in_=ln_g.rearrange("(j p) -> j p", p=P))
         nc.scalar.dma_start(out=ln_rows[K_TILES : 2 * K_TILES, :], in_=ln_b.rearrange("(j p) -> j p", p=P))
-        minus_half = keep.tile([P, 2], F32, name="minus_half")
+        minus_half = keep.tile([P, GROUP], F32, name="minus_half")
         nc.vector.memset(minus_half[:], -0.5)
         ident_f32 = keep.tile([P, P], F32, name="ident_f32")
         make_identity(nc, ident_f32[:])
@@ -92,8 +94,8 @@ def tile_gaublock_pb_kernel(
         ln_cols = keep.tile([P, 2 * K_TILES], F32, name="ln_cols")
         nc.vector.tensor_copy(out=ln_cols[:], in_=ln_ps[:, 0 : 2 * K_TILES])
 
-        xn_codes = keep.tile([P, PAIRS, PASSES, 2 * P], U32, name="xn_codes", align_bytes=64)
-        xn_scales = keep.tile([P, PAIRS, PASSES, 2 * P], U8, name="xn_scales", align_bytes=64)
+        xn_codes = keep.tile([P, GROUPS, PASSES, GROUP * P], U32, name="xn_codes", align_bytes=64)
+        xn_scales = keep.tile([P, GROUPS, PASSES, GROUP * P], U8, name="xn_scales", align_bytes=64)
         w_codes = keep.tile([P, PASSES, 2 * E], U32, name="w_codes", align_bytes=64)
         w_scales = keep.tile([P, PASSES, 2 * E], U8, name="w_scales", align_bytes=64)
         wz_codes = keep.tile([P, PASSES, S], U32, name="wz_codes", align_bytes=64)
@@ -105,65 +107,69 @@ def tile_gaublock_pb_kernel(
                 in_=src.rearrange("p t (a i) -> p a t i", i=4),
             )
 
-        def layer_norm(pair):
-            stats = stat.tile([P, 2, 2, 6], F32, name="stats")
-            mean_var = stat.tile([P, 2, 2], F32, name="mean_var")
-            for i in range(2):
+        def layer_norm(group):
+            first = GROUP * group
+            stats = stat.tile([P, GROUP, 2, 6], F32, name="stats")
+            mean_var = stat.tile([P, GROUP, 2], F32, name="mean_var")
+            for i in range(GROUP):
                 for h in range(2):
-                    nc.vector.bn_stats(out=stats[:, i, h, :], in_=x_sb[:, 2 * pair + i, 512 * h : 512 * (h + 1)])
+                    nc.vector.bn_stats(out=stats[:, i, h, :], in_=x_sb[:, first + i, 512 * h : 512 * (h + 1)])
                 nc.vector.bn_aggr(out=mean_var[:, i, :], in_=stats[:, i, :, :].rearrange("p a b -> p (a b)"))
-            var_eps = stat.tile([P, 2], F32, name="var_eps")
+            var_eps = stat.tile([P, GROUP], F32, name="var_eps")
             nc.vector.tensor_scalar_add(out=var_eps[:], in0=mean_var[:, :, 1], scalar1=LN_EPS)
-            neg_mean = stat.tile([P, 2], F32, name="neg_mean")
+            neg_mean = stat.tile([P, GROUP], F32, name="neg_mean")
             nc.vector.tensor_scalar_mul(out=neg_mean[:], in0=mean_var[:, :, 0], scalar1=-1.0)
-            rstd = stat.tile([P, 2], F32, name="rstd")
+            rstd = stat.tile([P, GROUP], F32, name="rstd")
             nc.gpsimd.tensor_tensor(out=rstd[:], in0=var_eps[:], in1=minus_half[:], op=ALU.pow)
             rows = []
-            for i in range(2):
+            for i in range(GROUP):
                 y = normed.tile([P, D], F32, name="y")
                 nc.gpsimd.tensor_scalar(
                     out=y[:],
-                    in0=x_sb[:, 2 * pair + i, :],
+                    in0=x_sb[:, first + i, :],
                     scalar1=neg_mean[:, i : i + 1],
                     scalar2=rstd[:, i : i + 1],
                     op0=ALU.add,
                     op1=ALU.mult,
                 )
                 rows.append(y)
-            k_tiles = stage.tile([P, K_TILES, 2 * P], BF16, name="k_tiles")
-            for a in range(K_TILES // 2):
-                turned = psum.tile([P, 2, 2 * P], F32, name="turned", tag="bank")
-                for b in range(2):
-                    j = 2 * a + b
-                    for i in range(2):
+            grouped = stage.tile([P, PASSES, GROUP * P, PACK], BF16, name="xn_grouped", align_bytes=64, bufs=1)
+            for c in range(PASSES):
+                k_tiles = stage.tile([P, PACK, GROUP * P], BF16, name="k_tiles")
+                banks = []
+                for t in range(PACK):
+                    banks.append(psum.tile([P, GROUP * P], F32, name="turned", tag="bank"))
+                for i in range(GROUP):
+                    for t in range(PACK):
+                        j = PACK * c + t
                         nc.tensor.transpose(
-                            out=turned[:, b, P * i : P * (i + 1)], in_=rows[i][:, P * j : P * (j + 1)], identity=ident_f32[:]
+                            out=banks[t][:, P * i : P * (i + 1)], in_=rows[i][:, P * j : P * (j + 1)], identity=ident_f32[:]
                         )
-                for b in range(2):
-                    j = 2 * a + b
+                for t in range(PACK):
+                    j = PACK * c + t
                     nc.scalar.activation(
-                        out=k_tiles[:, j, :],
-                        in_=turned[:, b, :],
+                        out=k_tiles[:, t, :],
+                        in_=banks[t][:],
                         func=ACT.Identity,
                         scale=ln_cols[:, j : j + 1],
                         bias=ln_cols[:, K_TILES + j : K_TILES + j + 1],
                     )
-            grouped = stage.tile([P, PASSES, 2 * P, PACK], BF16, name="xn_grouped", align_bytes=64)
-            for c in range(PASSES):
-                regroup(nc.scalar.copy, grouped[:, c, :, :], k_tiles[:, PACK * c : PACK * (c + 1), :])
+                regroup(nc.vector.tensor_copy, grouped[:, c, :, :], k_tiles[:])
             nc.vector.quantize_mx(
-                out=xn_codes[:, pair, :, :].rearrange("p c r -> p (c r)").bitcast(FP8X4),
-                scales=xn_scales[:, pair, :, :].rearrange("p c r -> p (c r)"),
+                out=xn_codes[:, group, :, :].rearrange("p c r -> p (c r)").bitcast(FP8X4),
+                scales=xn_scales[:, group, :, :].rearrange("p c r -> p (c r)"),
                 in_=grouped[:].rearrange("p c r t -> p (c r t)"),
             )
 
         def quantise_w(chunk):
             cols = slice(CHUNK * chunk, CHUNK * (chunk + 1))
+            half = CHUNK // 2
             grouped = []
-            for c, copy in enumerate((nc.vector.tensor_copy, nc.scalar.copy)):
-                g = stage.tile([P, CHUNK, PACK], BF16, name="w_grouped", align_bytes=64)
-                regroup(copy, g[:], w_raw[(chunk, c)][:])
-                grouped.append(g)
+            for c in range(PASSES):
+                grouped.append(stage.tile([P, CHUNK, PACK], BF16, name="w_grouped", align_bytes=64))
+            regroup(nc.vector.tensor_copy, grouped[0][:, 0:half, :], w_raw[(chunk, 0)][:, :, 0:half])
+            regroup(nc.scalar.copy, grouped[0][:, half:CHUNK, :], w_raw[(chunk, 0)][:, :, half:CHUNK])
+            regroup(nc.scalar.copy, grouped[1][:], w_raw[(chunk, 1)][:])
             for c in range(PASSES):
                 nc.vector.quantize_mx(
                     out=w_codes[:, c, cols].bitcast(FP8X4),
@@ -182,12 +188,12 @@ def tile_gaublock_pb_kernel(
             )
 
         def mx_group(acc, tile_m, rhs_codes, rhs_scales):
-            pair, i = tile_m // 2, tile_m % 2
+            group, i = tile_m // GROUP, tile_m % GROUP
             for c in range(PASSES):
                 nc.tensor.matmul_mx(
                     out=acc,
-                    lhsT=xn_codes[:, pair, c, P * i : P * (i + 1)].bitcast(FP8X4),
-                    lhsT_scale=xn_scales[:, pair, c, P * i : P * (i + 1)],
+                    lhsT=xn_codes[:, group, c, P * i : P * (i + 1)].bitcast(FP8X4),
+                    lhsT_scale=xn_scales[:, group, c, P * i : P * (i + 1)],
                     rhs=rhs_codes[c].bitcast(FP8X4),
                     rhs_scale=rhs_scales[c],
                     start=(c == 0),
@@ -244,10 +250,9 @@ def tile_gaublock_pb_kernel(
 
         layer_norm(0)
         quantise_w(0)
+        layer_norm(1)
         for pair in range(PAIRS):
-            if pair + 1 < PAIRS:
-                layer_norm(pair + 1)
-            else:
+            if pair == PAIRS // 2:
                 quantise_w(1)
             project(0, pair)
         for chunk in range(1, CHUNKS):

from contextlib import ExitStack

import concourse.mybir as mybir
from concourse.masks import make_identity

F32 = mybir.dt.float32
BF16 = mybir.dt.bfloat16
U32 = mybir.dt.uint32
U8 = mybir.dt.uint8
I32 = mybir.dt.int32
FP8X4 = mybir.dt.float8_e4m3fn_x4
ALU = mybir.AluOpType
ACT = mybir.ActivationFunctionType

P = 128
PACK = 4
PASSES = 2
ROWS = 1024
D = 1024
E = 2048
S = 128
F = E + E + S
ROW_TILES = ROWS // P
PAIRS = ROW_TILES // 2
GROUP = 4
GROUPS = ROW_TILES // GROUP
K_TILES = D // P
BANK = 512
CHUNK = 1024
CHUNKS = (E + E) // CHUNK
LN_EPS = 1e-5
FLOPS = 2 * ROWS * D * F


def tile_gaublock_pb_kernel(
    tc, x, ln_g, ln_b, W_in, b_in, gamma_q, beta_q, gamma_k, beta_k, out_0, out_1, out_2, out_3
):
    nc = tc.nc
    x_rows = x.flatten_outer_dims().rearrange("(p m) k -> p m k", m=ROW_TILES)
    w_rows = W_in.rearrange("(j p) n -> p j n", p=P)
    uv_rows = [out.flatten_outer_dims().rearrange("(p m) f -> p m f", m=ROW_TILES) for out in (out_0, out_1)]
    qk_rows = [out.flatten_outer_dims().rearrange("(p m) s -> p m s", m=ROW_TILES) for out in (out_2, out_3)]

    with ExitStack() as ctx:
        keep = ctx.enter_context(tc.tile_pool(name="keep", bufs=1))
        stat = ctx.enter_context(tc.tile_pool(name="stat", bufs=2))
        normed = ctx.enter_context(tc.tile_pool(name="normed", bufs=GROUP))
        stage = ctx.enter_context(tc.tile_pool(name="stage", bufs=2))
        result = ctx.enter_context(tc.tile_pool(name="result", bufs=4))
        psum = ctx.enter_context(tc.psum_pool(name="psum", bufs=8))

        ln_rows = keep.tile([P, P], BF16, name="ln_rows")
        nc.vector.memset(ln_rows[:].bitcast(I32), 0)
        nc.scalar.dma_start(out=ln_rows[0:K_TILES, :], in_=ln_g.rearrange("(j p) -> j p", p=P))
        nc.scalar.dma_start(out=ln_rows[K_TILES : 2 * K_TILES, :], in_=ln_b.rearrange("(j p) -> j p", p=P))
        minus_half = keep.tile([P, GROUP], F32, name="minus_half")
        nc.vector.memset(minus_half[:], -0.5)
        ident_f32 = keep.tile([P, P], F32, name="ident_f32")
        make_identity(nc, ident_f32[:])
        ident_bf16 = keep.tile([P, P], BF16, name="ident_bf16")
        nc.vector.tensor_copy(out=ident_bf16[:], in_=ident_f32[:])

        x_sb = keep.tile([P, ROW_TILES, D], BF16, name="x_sb")
        w_raw = {}
        bias_all = keep.tile([P, F], BF16, name="bias_all")
        qk_all = keep.tile([P, 4, S], BF16, name="qk_all")
        wz_raw = keep.tile([P, K_TILES, S], BF16, name="wz_raw")

        def load_x(pair):
            nc.sync.dma_start(out=x_sb[:, 2 * pair : 2 * pair + 2, :], in_=x_rows[:, 2 * pair : 2 * pair + 2, :])

        def load_w(chunk):
            for c in range(PASSES):
                raw = keep.tile([P, PACK, CHUNK], BF16, name="w_raw%d_%d" % (chunk, c))
                nc.sync.dma_start(
                    out=raw[:], in_=w_rows[:, PACK * c : PACK * (c + 1), CHUNK * chunk : CHUNK * (chunk + 1)]
                )
                w_raw[(chunk, c)] = raw

        load_x(0)
        load_x(1)
        load_w(0)
        load_x(2)
        load_x(3)
        nc.sync.dma_start(out=bias_all[:], in_=b_in.partition_broadcast(P))
        for chunk in range(1, CHUNKS):
            load_w(chunk)
        nc.sync.dma_start(out=wz_raw[:], in_=w_rows[:, :, 2 * E : F])
        for i, vec in enumerate((gamma_q, beta_q, gamma_k, beta_k)):
            nc.sync.dma_start(out=qk_all[:, i, :], in_=vec.partition_broadcast(P))

        ln_ps = psum.tile([P, P], F32, name="ln_ps", tag="bank")
        nc.tensor.matmul(out=ln_ps[:], lhsT=ln_rows[:], rhs=ident_bf16[:], start=True, stop=True)
        ln_cols = keep.tile([P, 2 * K_TILES], F32, name="ln_cols")
        nc.vector.tensor_copy(out=ln_cols[:], in_=ln_ps[:, 0 : 2 * K_TILES])

        xn_codes = keep.tile([P, GROUPS, PASSES, GROUP * P], U32, name="xn_codes", align_bytes=64)
        xn_scales = keep.tile([P, GROUPS, PASSES, GROUP * P], U8, name="xn_scales", align_bytes=64)
        w_codes = keep.tile([P, PASSES, 2 * E], U32, name="w_codes", align_bytes=64)
        w_scales = keep.tile([P, PASSES, 2 * E], U8, name="w_scales", align_bytes=64)
        wz_codes = keep.tile([P, PASSES, S], U32, name="wz_codes", align_bytes=64)
        wz_scales = keep.tile([P, PASSES, S], U8, name="wz_scales", align_bytes=64)

        def regroup(copy, dst, src):
            copy(
                out=dst.rearrange("p (a i) t -> p a t i", i=4),
                in_=src.rearrange("p t (a i) -> p a t i", i=4),
            )

        def layer_norm(group):
            first = GROUP * group
            stats = stat.tile([P, GROUP, 2, 6], F32, name="stats")
            mean_var = stat.tile([P, GROUP, 2], F32, name="mean_var")
            for i in range(GROUP):
                for h in range(2):
                    nc.vector.bn_stats(out=stats[:, i, h, :], in_=x_sb[:, first + i, 512 * h : 512 * (h + 1)])
                nc.vector.bn_aggr(out=mean_var[:, i, :], in_=stats[:, i, :, :].rearrange("p a b -> p (a b)"))
            var_eps = stat.tile([P, GROUP], F32, name="var_eps")
            nc.vector.tensor_scalar_add(out=var_eps[:], in0=mean_var[:, :, 1], scalar1=LN_EPS)
            neg_mean = stat.tile([P, GROUP], F32, name="neg_mean")
            nc.vector.tensor_scalar_mul(out=neg_mean[:], in0=mean_var[:, :, 0], scalar1=-1.0)
            rstd = stat.tile([P, GROUP], F32, name="rstd")
            nc.gpsimd.tensor_tensor(out=rstd[:], in0=var_eps[:], in1=minus_half[:], op=ALU.pow)
            rows = []
            for i in range(GROUP):
                y = normed.tile([P, D], F32, name="y")
                nc.gpsimd.tensor_scalar(
                    out=y[:],
                    in0=x_sb[:, first + i, :],
                    scalar1=neg_mean[:, i : i + 1],
                    scalar2=rstd[:, i : i + 1],
                    op0=ALU.add,
                    op1=ALU.mult,
                )
                rows.append(y)
            grouped = stage.tile([P, PASSES, GROUP * P, PACK], BF16, name="xn_grouped", align_bytes=64, bufs=1)
            for c in range(PASSES):
                k_tiles = stage.tile([P, PACK, GROUP * P], BF16, name="k_tiles")
                banks = []
                for t in range(PACK):
                    banks.append(psum.tile([P, GROUP * P], F32, name="turned", tag="bank"))
                for i in range(GROUP):
                    for t in range(PACK):
                        j = PACK * c + t
                        nc.tensor.transpose(
                            out=banks[t][:, P * i : P * (i + 1)], in_=rows[i][:, P * j : P * (j + 1)], identity=ident_f32[:]
                        )
                for t in range(PACK):
                    j = PACK * c + t
                    nc.scalar.activation(
                        out=k_tiles[:, t, :],
                        in_=banks[t][:],
                        func=ACT.Identity,
                        scale=ln_cols[:, j : j + 1],
                        bias=ln_cols[:, K_TILES + j : K_TILES + j + 1],
                    )
                regroup(nc.vector.tensor_copy, grouped[:, c, :, :], k_tiles[:])
            nc.vector.quantize_mx(
                out=xn_codes[:, group, :, :].rearrange("p c r -> p (c r)").bitcast(FP8X4),
                scales=xn_scales[:, group, :, :].rearrange("p c r -> p (c r)"),
                in_=grouped[:].rearrange("p c r t -> p (c r t)"),
            )

        def quantise_w(chunk):
            cols = slice(CHUNK * chunk, CHUNK * (chunk + 1))
            half = CHUNK // 2
            grouped = []
            for c in range(PASSES):
                grouped.append(stage.tile([P, CHUNK, PACK], BF16, name="w_grouped", align_bytes=64))
            regroup(nc.vector.tensor_copy, grouped[0][:, 0:half, :], w_raw[(chunk, 0)][:, :, 0:half])
            regroup(nc.scalar.copy, grouped[0][:, half:CHUNK, :], w_raw[(chunk, 0)][:, :, half:CHUNK])
            regroup(nc.scalar.copy, grouped[1][:], w_raw[(chunk, 1)][:])
            for c in range(PASSES):
                nc.vector.quantize_mx(
                    out=w_codes[:, c, cols].bitcast(FP8X4),
                    scales=w_scales[:, c, cols],
                    in_=grouped[c][:].rearrange("p n t -> p (n t)"),
                )

        def quantise_wz():
            grouped = keep.tile([P, PASSES, S, PACK], BF16, name="wz_grouped", align_bytes=64)
            for c in range(PASSES):
                regroup(nc.scalar.copy, grouped[:, c, :, :], wz_raw[:, PACK * c : PACK * (c + 1), :])
            nc.vector.quantize_mx(
                out=wz_codes[:].rearrange("p c n -> p (c n)").bitcast(FP8X4),
                scales=wz_scales[:].rearrange("p c n -> p (c n)"),
                in_=grouped[:].rearrange("p c n t -> p (c n t)"),
            )

        def mx_group(acc, tile_m, rhs_codes, rhs_scales):
            group, i = tile_m // GROUP, tile_m % GROUP
            for c in range(PASSES):
                nc.tensor.matmul_mx(
                    out=acc,
                    lhsT=xn_codes[:, group, c, P * i : P * (i + 1)].bitcast(FP8X4),
                    lhsT_scale=xn_scales[:, group, c, P * i : P * (i + 1)],
                    rhs=rhs_codes[c].bitcast(FP8X4),
                    rhs_scale=rhs_scales[c],
                    start=(c == 0),
                    stop=(c == PASSES - 1),
                )

        def project(chunk, pair):
            out_sb = result.tile([P, 2, CHUNK], F32, name="out_sb")
            for i in range(2):
                for h in range(CHUNK // BANK):
                    cols = slice(CHUNK * chunk + BANK * h, CHUNK * chunk + BANK * (h + 1))
                    acc = psum.tile([P, BANK], F32, name="acc", tag="bank")
                    mx_group(
                        acc[:],
                        2 * pair + i,
                        [w_codes[:, c, cols] for c in range(PASSES)],
                        [w_scales[:, c, cols] for c in range(PASSES)],
                    )
                    nc.vector.tensor_tensor(
                        out=out_sb[:, i, BANK * h : BANK * (h + 1)], in0=acc[:], in1=bias_all[:, cols], op=ALU.add
                    )
            nc.scalar.activation(out=out_sb[:], in_=out_sb[:], func=ACT.Silu)
            first = (CHUNK * chunk) % E
            nc.sync.dma_start(
                out=uv_rows[(CHUNK * chunk) // E][:, 2 * pair : 2 * pair + 2, first : first + CHUNK], in_=out_sb[:]
            )

        def project_z():
            z_sb = result.tile([P, ROW_TILES, S], F32, name="z_sb", tag="out_sb")
            per_bank = BANK // S
            for a in range(ROW_TILES // per_bank):
                acc = psum.tile([P, per_bank, S], F32, name="acc_z", tag="bank")
                for i in range(per_bank):
                    mx_group(
                        acc[:, i, :],
                        per_bank * a + i,
                        [wz_codes[:, c, :] for c in range(PASSES)],
                        [wz_scales[:, c, :] for c in range(PASSES)],
                    )
                nc.vector.tensor_tensor(
                    out=z_sb[:, per_bank * a : per_bank * (a + 1), :],
                    in0=acc[:],
                    in1=bias_all[:, 2 * E : F].unsqueeze(1).to_broadcast([P, per_bank, S]),
                    op=ALU.add,
                )
            nc.scalar.activation(out=z_sb[:], in_=z_sb[:], func=ACT.Silu)
            for w in range(2):
                gain = qk_all[:, 2 * w, :].unsqueeze(1).to_broadcast([P, ROW_TILES, S])
                offset = qk_all[:, 2 * w + 1, :].unsqueeze(1).to_broadcast([P, ROW_TILES, S])
                mapped = result.tile([P, ROW_TILES, S], F32, name="mapped", tag="out_sb")
                nc.gpsimd.tensor_tensor(out=mapped[:], in0=z_sb[:], in1=gain, op=ALU.mult)
                nc.gpsimd.tensor_tensor(out=mapped[:], in0=mapped[:], in1=offset, op=ALU.add)
                nc.sync.dma_start(out=qk_rows[w], in_=mapped[:])

        layer_norm(0)
        quantise_w(0)
        layer_norm(1)
        for pair in range(PAIRS):
            if pair == PAIRS // 2:
                quantise_w(1)
            project(0, pair)
        for chunk in range(1, CHUNKS):
            if chunk + 1 < CHUNKS:
                quantise_w(chunk + 1)
            else:
                quantise_wz()
                project_z()
            for pair in range(PAIRS):
                project(chunk, pair)
